import numpy as np
import ml_dtypes


def mxq(x, axis, fmt="e4m3"):
    dtype, down = {"e4m3": (ml_dtypes.float8_e4m3fn, 7), "e5m2": (ml_dtypes.float8_e5m2, 14)}[fmt]
    v = np.moveaxis(np.asarray(x, np.float32).astype(ml_dtypes.bfloat16).astype(np.float64), axis, -1)
    blocks = v.reshape(v.shape[:-1] + (-1, 32))
    amax = np.abs(blocks).max(-1, keepdims=True)
    byte = np.maximum(np.where(amax > 0, np.frexp(amax)[1] - 1 + 127, 0) - down, 1)
    scale = np.exp2(byte - 127.0)
    codes = (blocks / scale).astype(np.float32).astype(dtype).astype(np.float64)
    return np.moveaxis((codes * scale).reshape(v.shape), -1, axis)


WIDE = False


def mx_kscale(k):
    if not WIDE:
        return np.ones(k)
    levels = np.array([10, -10, 5, -5, 0])
    if k % 512:
        return np.exp2(np.random.permutation(np.resize(levels, k // 32))).repeat(32)
    a = np.empty((k // 512, 16))
    for p in range(k // 512):
        a[p, :8] = np.random.permutation(np.resize(levels, 8))
        for g in range(8):
            far = levels[np.abs(levels - a[p, g]) >= 10]
            a[p, g + 8] = far[np.random.randint(len(far))]
    return np.exp2(a.ravel()).repeat(32)


BF16 = ml_dtypes.bfloat16


def bf(x):
    return np.asarray(x, np.float32).astype(BF16)


def f64(x):
    return np.asarray(x).astype(np.float64)


B, D, OUT = 1024, 1024, 2048

TINY = 1e-15


def _arg_v(x, z, r, bias):
    zn = np.maximum(np.sqrt(np.sum(z * z, axis=1)), TINY)
    sr = np.clip(r[:, 0], -15.0, 15.0)
    beta = np.sqrt(1.0 + np.sum(x * x, axis=1, keepdims=True))
    xz = x @ z.T
    a = np.clip((np.cosh(sr)[None, :] * xz - (np.sinh(sr) * zn)[None, :] * beta) / zn[None, :], -1e6, 1e6)
    v = zn[None, :] * np.arcsinh(a) + bias[None, :]
    return a, v


def setup_inputs():
    s = mx_kscale(B)
    s = (s / np.min(s))[:, None]
    u = mx_kscale(OUT)
    x0 = bf(np.random.standard_normal((B, D)))
    z0 = bf(np.random.standard_normal((OUT, D)) * 0.5 / np.sqrt(D))
    r = bf(np.random.uniform(-1.0, 1.0, (OUT, 1)) * 4.0 / np.sqrt(D))
    bias = bf(np.random.standard_normal(OUT) * 0.1)
    g = bf(np.random.standard_normal((B, OUT)) * np.exp2(np.random.randint(-6, 1, (B, 1))) * 4.0 / s * u)
    a, v = _arg_v(f64(x0), f64(z0), f64(r), f64(bias))
    return {"x": bf(f64(x0) * s), "z": bf(f64(z0) / u[:, None]), "r": r, "bias": bias,
            "arg": np.asarray(a, np.float32), "v": np.asarray(v, np.float32), "grad_out": g}


def reference(x, z, r, bias, arg, v, grad_out):
    xf = f64(x)
    zf = f64(z)
    a = f64(arg)
    sr = f64(r)[:, 0]
    c = np.cosh(sr)[None, :]
    sh = np.sinh(sr)[None, :]
    zn = np.sqrt(np.sum(zf * zf, axis=1))[None, :]
    beta = np.sqrt(1.0 + np.sum(xf * xf, axis=1, keepdims=True))
    dv = f64(grad_out) * np.cosh(f64(v))
    h = dv / np.sqrt(1.0 + a * a)
    dxz = h * c
    dbeta = -np.sum(h * (zn * sh), axis=1, keepdims=True)
    t = np.sum(dv * np.arcsinh(a) - h * (a + sh * beta), axis=0)
    dx = (mxq(dxz, 1, "e5m2") @ mxq(zf, 0, "e4m3")) + dbeta * xf / beta
    dw = (mxq(dxz, 0, "e5m2").T @ mxq(xf, 0, "e4m3")) + zf * (t / zn[0])[:, None]
    return dx, dw

@@ -1,0 +1,577 @@
+from contextlib import ExitStack
+
+import concourse.mybir as mybir
+from concourse.masks import make_identity
+
+B, D, OUT = 1024, 1024, 2048
+FLOPS = 2 * 2 * B * D * OUT
+
+F32 = mybir.dt.float32
+BF16 = mybir.dt.bfloat16
+U32 = mybir.dt.uint32
+U8 = mybir.dt.uint8
+E4 = mybir.dt.float8_e4m3fn_x4
+E5 = mybir.dt.float8_e5m2_x4
+ALU = mybir.AluOpType
+ACT = mybir.ActivationFunctionType
+AX = mybir.AxisListType
+
+P = 128
+CH = 512
+NG = OUT // CH
+AW = 136
+
+
+def tile_pvfc_v_kernel(tc, x, z, r, bias, arg, v, grad_out, out_0, out_1):
+    nc = tc.nc
+    arg_v = arg.rearrange("(g p j) o -> g p j o", g=2, j=4)
+    v_v = v.rearrange("(g p j) o -> g p j o", g=2, j=4)
+    go_v = grad_out.rearrange("(g p j) o -> g p j o", g=2, j=4)
+    x_v = x.rearrange("(g p j) d -> g p j d", g=2, j=4)
+    o0_v = out_0.rearrange("(g p j) d -> g p j d", g=2, j=4)
+    zq_v = z.rearrange("(c p j) d -> c p j d", c=NG, j=4)
+    zn_v = z.rearrange("(c m p) d -> c p m d", c=NG, m=4)
+    o1_v = out_1.rearrange("(c m p) d -> c p m d", c=NG, m=4)
+
+    with ExitStack() as ctx:
+        ctx.enter_context(tc.manual_schedule())
+        keep = ctx.enter_context(tc.tile_pool(name="keep", bufs=1))
+        strm = ctx.enter_context(tc.tile_pool(name="strm", bufs=2))
+        psum = ctx.enter_context(tc.psum_pool(name="psum", bufs=1))
+
+        ident = keep.tile([P, P], F32, name="ident")
+        make_identity(nc, ident[:])
+        one_c = keep.tile([P, 1], F32, name="one_c")
+        nc.vector.memset(one_c[:], 1.0)
+
+        x_codes = keep.tile([P, 2, D], U32, name="x_codes", align_bytes=64)
+        x_scales = keep.tile([P, 2, D], U8, name="x_scales", align_bytes=64)
+        z_codes = keep.tile([P, NG, D], U32, name="z_codes", align_bytes=64)
+        z_scales = keep.tile([P, NG, D], U8, name="z_scales", align_bytes=64)
+        ft_codes = keep.tile([P, NG, B], U32, name="ft_codes", align_bytes=64)
+        ft_scales = keep.tile([P, NG, B], U8, name="ft_scales", align_bytes=64)
+        r_bc = keep.tile([P, OUT], BF16, name="r_bc")
+
+        xs = keep.tile([P, 8], F32, name="xs")
+        beta = keep.tile([P, 8], F32, name="beta")
+        rbeta = keep.tile([P, 8], F32, name="rbeta")
+        zs2 = keep.tile([P, 4 * NG], F32, name="zs2")
+        zn = keep.tile([P, 4 * NG], F32, name="zn")
+        rzn = keep.tile([P, 4 * NG], F32, name="rzn")
+        shn = keep.tile([P, 4 * NG], F32, name="shn")
+        dbp = keep.tile([P, 8, NG], F32, name="dbp")
+        sums = keep.tile([P, 2 * NG, 12], F32, name="sums")
+        sb = keep.tile([P, 8], F32, name="sb")
+
+        A, V, GT, Q, M, WT, E2, SG = {}, {}, {}, {}, {}, {}, {}, {}
+        CHALF, ZSN, SHH, ER, TK, TKS, D16, GRP, TP, DG, MINI = {}, {}, {}, {}, {}, {}, {}, {}, {}, {}, {}
+        ZT = {}
+
+        def cols(c):
+            return slice(CH * c, CH * (c + 1))
+
+        def load_a(c, k):
+            A[(c, k)] = strm.tile([P, 2, 4, AW], F32, name="A", bufs=6)
+            for jj in range(2):
+                nc.sync.dma_start(
+                    out=A[(c, k)][:, jj, :, 0:P],
+                    in_=arg_v[k // 2][:, 2 * (k % 2) + jj, cols(c)].rearrange("p (m o) -> p m o", m=4),
+                )
+
+        def fill_beta(c, k):
+            nc.gpsimd.tensor_copy(
+                out=A[(c, k)][:, :, :, P : P + 1],
+                in_=beta[:, 2 * k : 2 * k + 2].unsqueeze(2).unsqueeze(3).to_broadcast([P, 2, 4, 1]),
+            )
+
+        def blocks(t):
+            return t[:].rearrange("p j (m o) -> p j m o", m=4)
+
+        def load_vg(c, k):
+            V[(c, k)] = strm.tile([P, 2, CH], F32, name="V", bufs=4)
+            nc.sync.dma_start(out=V[(c, k)][:], in_=v_v[k // 2][:, 2 * (k % 2) : 2 * (k % 2) + 2, cols(c)])
+            GT[(c, k)] = strm.tile([P, 2, CH], BF16, name="GT", bufs=4)
+            nc.sync.dma_start(out=GT[(c, k)][:], in_=go_v[k // 2][:, 2 * (k % 2) : 2 * (k % 2) + 2, cols(c)])
+
+        def load_zt(c, m):
+            ZT[(c, m)] = strm.tile([P, D], BF16, name="ZT", bufs=4)
+            nc.sync.dma_start(out=ZT[(c, m)][:], in_=zn_v[c][:, m, :])
+
+        def s_phase(c, k):
+            Q[(c, k)] = strm.tile([P, 2, CH], F32, name="Q", bufs=6)
+            WT[(c, k)] = strm.tile([P, 2, CH], F32, name="WT", bufs=2)
+            M[(c, k)] = strm.tile([P, 2, CH], F32, name="M", bufs=6)
+            nc.scalar.activation(out=blocks(Q[(c, k)]), in_=A[(c, k)][:, :, :, 0:P], func=ACT.Square)
+            nc.scalar.activation(out=WT[(c, k)][:], in_=Q[(c, k)][:], func=ACT.Sqrt, bias=one_c[:])
+            nc.scalar.activation(out=blocks(M[(c, k)]), in_=A[(c, k)][:, :, :, 0:P], func=ACT.Abs)
+
+        def u_op(c, k):
+            nc.vector.tensor_tensor(out=M[(c, k)][:], in0=M[(c, k)][:], in1=WT[(c, k)][:], op=ALU.add)
+
+        def zn_squares(c):
+            for m in range(4):
+                sq = strm.tile([P, D], BF16, name="sq", bufs=1)
+                nc.scalar.activation(
+                    out=sq[:], in_=ZT[(c, m)][:], func=ACT.Square, accum_out=zs2[:, 4 * c + m : 4 * c + m + 1]
+                )
+
+        def zn_sqrt(c):
+            nc.scalar.activation(out=zn[:, 4 * c : 4 * c + 4], in_=zs2[:, 4 * c : 4 * c + 4], func=ACT.Sqrt)
+
+        def r_phase(c, k):
+            nc.scalar.activation(out=Q[(c, k)][:], in_=Q[(c, k)][:], func=ACT.Abs_reciprocal_sqrt, bias=one_c[:])
+
+        def l_phase(c, k):
+            nc.scalar.activation(out=M[(c, k)][:], in_=M[(c, k)][:], func=ACT.Ln)
+
+        def e_r(c):
+            ER[(c, 0)] = strm.tile([P, CH], F32, name="ER0", bufs=1)
+            ER[(c, 1)] = strm.tile([P, CH], F32, name="ER1", bufs=1)
+            nc.scalar.activation(out=ER[(c, 0)][:], in_=r_bc[:, cols(c)], func=ACT.Exp)
+            nc.scalar.activation(out=ER[(c, 1)][:], in_=r_bc[:, cols(c)], func=ACT.Exp, scale=-1.0)
+
+        def e_phase(c, k):
+            E2[(c, k)] = strm.tile([P, 2, CH], F32, name="E2", bufs=2)
+            nc.scalar.activation(out=E2[(c, k)][:], in_=V[(c, k)][:], func=ACT.Exp, scale=-1.0)
+            nc.scalar.activation(out=V[(c, k)][:], in_=V[(c, k)][:], func=ACT.Exp)
+
+        def sign_phase(c, k):
+            SG[(c, k)] = strm.tile([P, 2, CH], BF16, name="SG", bufs=2)
+            nc.scalar.activation(out=blocks(SG[(c, k)]), in_=A[(c, k)][:, :, :, 0:P], func=ACT.Sign)
+
+        def cz_pe(c):
+            bc = psum.tile([P, CH], F32, name="mx", bufs=3)
+            for m in range(4):
+                nc.tensor.matmul(
+                    out=bc[:, P * m : P * (m + 1)],
+                    lhsT=zn[:, 4 * c + m : 4 * c + m + 1].to_broadcast([P, P]),
+                    rhs=ident[:],
+                    start=True,
+                    stop=True,
+                )
+            return bc
+
+        def cz_dve1(c):
+            CHALF[c] = strm.tile([P, CH], F32, name="CHALF", bufs=2)
+            SHH[c] = strm.tile([P, CH], F32, name="SHH", bufs=1)
+            nc.vector.tensor_tensor(out=CHALF[c][:], in0=ER[(c, 0)][:], in1=ER[(c, 1)][:], op=ALU.add)
+            nc.vector.tensor_tensor(out=SHH[c][:], in0=ER[(c, 1)][:], in1=ER[(c, 0)][:], op=ALU.subtract)
+            nc.vector.tensor_scalar(out=CHALF[c][:], in0=CHALF[c][:], scalar1=0.5, scalar2=None, op0=ALU.mult)
+            nc.vector.tensor_scalar(out=SHH[c][:], in0=SHH[c][:], scalar1=0.5, scalar2=None, op0=ALU.mult)
+            nc.vector.reciprocal(out=rzn[:, 4 * c : 4 * c + 4], in_=zn[:, 4 * c : 4 * c + 4])
+
+        def cz_pe2(c):
+            mn = psum.tile([P, CH], F32, name="mx", bufs=3)
+            for m in range(4):
+                nc.tensor.matmul(
+                    out=mn[:, m : m + 1], lhsT=SHH[c][:, P * m : P * (m + 1)], rhs=ident[:, 0:1], start=True, stop=True
+                )
+            return mn
+
+        def cz_dve2(c, bc, mn):
+            ZSN[c] = strm.tile([P, CH], F32, name="ZSN", bufs=2)
+            nc.vector.tensor_tensor(out=ZSN[c][:], in0=bc[:], in1=SHH[c][:], op=ALU.mult)
+            nc.vector.tensor_copy(out=shn[:, 4 * c : 4 * c + 4], in_=mn[:, 0:4])
+
+        def chain_steps(c, k):
+            sg, vv, g2, q, mm, e2 = SG[(c, k)], V[(c, k)], GT[(c, k)], Q[(c, k)], M[(c, k)], E2[(c, k)]
+            h, jp = k // 2, k % 2
+            d16 = D16[(c, h)]
+
+            def dbeta_step(jj):
+                junk = late.tile([P, CH], BF16, name="junk", bufs=1)
+                s = 4 * h + 2 * jp + jj
+                nc.vector.scalar_tensor_tensor(
+                    out=junk[:], in0=q[:, jj, :], scalar=1.0, in1=ZSN[c][:], op0=ALU.mult, op1=ALU.mult,
+                    accum_out=dbp[:, s, c : c + 1],
+                )
+
+            return [
+                lambda: nc.vector.tensor_tensor(out=vv[:], in0=vv[:], in1=e2[:], op=ALU.add),
+                lambda: nc.vector.scalar_tensor_tensor(
+                    out=vv[:], in0=vv[:], scalar=0.5, in1=g2[:], op0=ALU.mult, op1=ALU.mult
+                ),
+                lambda: nc.vector.tensor_tensor(out=q[:], in0=vv[:], in1=q[:], op=ALU.mult),
+                lambda: nc.vector.tensor_tensor(
+                    out=d16[:, 2 * jp : 2 * jp + 2, :], in0=q[:],
+                    in1=CHALF[c][:].unsqueeze(1).to_broadcast([P, 2, CH]), op=ALU.mult,
+                ),
+                lambda: nc.vector.tensor_tensor(out=mm[:], in0=vv[:], in1=mm[:], op=ALU.mult),
+                lambda: dbeta_step(0),
+                lambda: nc.vector.tensor_tensor(out=mm[:], in0=mm[:], in1=sg[:], op=ALU.mult),
+                lambda: dbeta_step(1),
+            ]
+
+        def chain_pair(c, h, first, last, between):
+            if first == 0:
+                D16[(c, h)] = late.tile([P, 4, CH], BF16, name="D16", bufs=2)
+            s0, s1 = chain_steps(c, 2 * h), chain_steps(c, 2 * h + 1)
+            for i in range(first, last):
+                s0[i]()
+                if between is not None:
+                    between(2 * (i - first))
+                s1[i]()
+                if between is not None:
+                    between(2 * (i - first) + 1)
+
+        def pe_transposes(c, h):
+            for jp in range(2):
+                TP[(c, h, jp)] = psum.tile([P, 4, P], F32, name="tp", bufs=2)
+                for jj in range(2):
+                    words = D16[(c, h)][:, 2 * jp + jj, :].bitcast(F32)
+                    for u in range(2):
+                        nc.tensor.transpose(out=TP[(c, h, jp)][:, 2 * jj + u, :], in_=words[:, u::2], identity=ident[:])
+
+        def evac(c, h):
+            GRP[(c, h)] = late.tile([P, CH, 4], BF16, name="GRP", bufs=1, align_bytes=64)
+            gw = GRP[(c, h)][:].rearrange("p t e -> p (t e)").bitcast(F32).rearrange("p (j r u) -> p j r u", j=4, u=2)
+            for jp in range(2):
+                nc.scalar.copy(
+                    out=gw[:, 2 * jp : 2 * jp + 2, :, :],
+                    in_=TP[(c, h, jp)][:].rearrange("p (jj u) r -> p jj r u", u=2),
+                )
+
+        def pe_diag(c, h):
+            for m in range(4):
+                blk = slice(P * m, P * (m + 1))
+                if m % 2 == 0:
+                    DG[(c, h, m // 2)] = psum.tile([P, 2, AW], F32, name="dg", bufs=2)
+                for j in range(4):
+                    k = 2 * h + j // 2
+                    nc.tensor.matmul(
+                        out=DG[(c, h, m // 2)][:, m % 2, 0 : P + 1], lhsT=Q[(c, k)][:, j % 2, blk],
+                        rhs=A[(c, k)][:, j % 2, m, 0 : P + 1], start=(j == 0), stop=(j == 3),
+                    )
+
+        def pe_minis(c, h):
+            MINI[(c, h)] = psum.tile([P, 16], F32, name="mini", bufs=1)
+            for m in range(4):
+                blk = slice(P * m, P * (m + 1))
+                for j in range(4):
+                    k = 2 * h + j // 2
+                    nc.tensor.matmul(
+                        out=MINI[(c, h)][:, m : m + 1], lhsT=M[(c, k)][:, j % 2, blk], rhs=one_c[:],
+                        start=(j == 0), stop=(j == 3),
+                    )
+
+        def post_tk(c, h):
+            if h == 0:
+                TK[c] = strm.tile([P, 2, CH], U32, name="TK", bufs=2, align_bytes=64)
+                TKS[c] = strm.tile([P, 2, CH], U8, name="TKS", bufs=2, align_bytes=64)
+            di = late.tile([P, CH, 4], BF16, name="DI", bufs=1, align_bytes=64)
+            nc.vector.tensor_copy(out=di[:], in_=D16[(c, h)][:].rearrange("p j o -> p o j"))
+            return di
+
+        def post_tk_q(c, h, di):
+            nc.vector.quantize_mx(
+                out=TK[c][:, h, :].bitcast(E5), scales=TKS[c][:, h, :], in_=di[:].rearrange("p o j -> p (o j)")
+            )
+
+        def post_ft_q(c, h):
+            nc.vector.quantize_mx(
+                out=ft_codes[:, c, CH * h : CH * (h + 1)].bitcast(E5), scales=ft_scales[:, c, CH * h : CH * (h + 1)],
+                in_=GRP[(c, h)][:].rearrange("p t e -> p (t e)"),
+            )
+
+        def post_sums(c, h):
+            for m in range(4):
+                jk = late.tile([P, P], F32, name="jk", bufs=1)
+                nc.vector.scalar_tensor_tensor(
+                    out=jk[:], in0=DG[(c, h, m // 2)][:, m % 2, 0:P], scalar=1.0, in1=ident[:], op0=ALU.mult,
+                    op1=ALU.mult, accum_out=sums[:, 2 * c + h, 8 + m : 9 + m],
+                )
+            for mp in range(2):
+                nc.vector.tensor_copy(
+                    out=sums[:, 2 * c + h, 4 + 2 * mp : 6 + 2 * mp], in_=DG[(c, h, mp)][:, :, P : P + 1].rearrange("p m one -> p (m one)")
+                )
+            nc.vector.tensor_copy(out=sums[:, 2 * c + h, 0:4], in_=MINI[(c, h)][:, 0:4])
+
+        def fin_small(c):
+            s12 = keep.tile([P, 12], F32, name="s12", bufs=2)
+            ta = keep.tile([P, 4], F32, name="ta", bufs=2)
+            tb = keep.tile([P, 4], F32, name="tb", bufs=2)
+            tz = keep.tile([P, 4], F32, name="tz", bufs=2)
+            nc.gpsimd.tensor_tensor(out=s12[:], in0=sums[:, 2 * c, :], in1=sums[:, 2 * c + 1, :], op=ALU.add)
+            nc.gpsimd.tensor_tensor(out=ta[:], in0=s12[:, 0:4], in1=s12[:, 8:12], op=ALU.subtract)
+            nc.gpsimd.tensor_tensor(out=tb[:], in0=s12[:, 4:8], in1=shn[:, 4 * c : 4 * c + 4], op=ALU.mult)
+            nc.gpsimd.tensor_tensor(out=ta[:], in0=ta[:], in1=tb[:], op=ALU.add)
+            nc.gpsimd.tensor_tensor(out=tz[:], in0=ta[:], in1=rzn[:, 4 * c : 4 * c + 4], op=ALU.mult)
+            return tz
+
+        PS, OST, XE = {}, {}, {}
+
+        def out1_pe(c, i):
+            m, dh = i // 2, i % 2
+            PS[("o1", c, i)] = psum.tile([P, 512], F32, name="mx", bufs=3)
+            for g in range(2):
+                nc.tensor.matmul_mx(
+                    out=PS[("o1", c, i)][:],
+                    lhsT=TK[c][:, g, P * m : P * (m + 1)].bitcast(E5),
+                    lhsT_scale=TKS[c][:, g, P * m : P * (m + 1)],
+                    rhs=x_codes[:, g, 512 * dh : 512 * (dh + 1)].bitcast(E4),
+                    rhs_scale=x_scales[:, g, 512 * dh : 512 * (dh + 1)],
+                    start=(g == 0), stop=(g == 1),
+                )
+
+        def out1_dve(c, i):
+            m, dh = i // 2, i % 2
+            if dh == 0:
+                OST[("o1", c, m)] = late.tile([P, D], F32, name="ost", bufs=2)
+            ost = OST[("o1", c, m)]
+            nc.vector.scalar_tensor_tensor(
+                out=ost[:, 512 * dh : 512 * (dh + 1)], in0=ZT[(c, m)][:, 512 * dh : 512 * (dh + 1)],
+                scalar=TZ[c][:, m : m + 1], in1=PS[("o1", c, i)][:], op0=ALU.mult, op1=ALU.add,
+            )
+            if dh == 1:
+                nc.sync.dma_start(out=o1_v[c][:, m, :], in_=ost[:])
+
+        def load_xe(g, j):
+            XE[(g, j)] = late.tile([P, D], BF16, name="xe", bufs=2)
+            nc.sync.dma_start(out=XE[(g, j)][:], in_=x_v[g][:, j, :])
+
+        def out0_scale(g):
+            dbs = keep.tile([P, 4], F32, name="dbs", bufs=2)
+            nc.vector.tensor_reduce(out=dbs[:], in_=dbp[:, 4 * g : 4 * g + 4, :], axis=AX.X, op=ALU.add)
+            nc.vector.tensor_tensor(out=sb[:, 4 * g : 4 * g + 4], in0=dbs[:], in1=rbeta[:, 4 * g : 4 * g + 4], op=ALU.mult)
+
+        def out0_pe(g, i):
+            s, dh = 4 * g + i // 2, i % 2
+            PS[("o0", g, i)] = psum.tile([P, 512], F32, name="mx", bufs=3)
+            for c in range(NG):
+                nc.tensor.matmul_mx(
+                    out=PS[("o0", g, i)][:],
+                    lhsT=ft_codes[:, c, P * s : P * (s + 1)].bitcast(E5),
+                    lhsT_scale=ft_scales[:, c, P * s : P * (s + 1)],
+                    rhs=z_codes[:, c, 512 * dh : 512 * (dh + 1)].bitcast(E4),
+                    rhs_scale=z_scales[:, c, 512 * dh : 512 * (dh + 1)],
+                    start=(c == 0), stop=(c == NG - 1),
+                )
+
+        def out0_dve(g, i):
+            j, dh = i // 2, i % 2
+            if dh == 0:
+                OST[("o0", g, j)] = late.tile([P, D], F32, name="ost", bufs=2)
+            ost = OST[("o0", g, j)]
+            nc.vector.scalar_tensor_tensor(
+                out=ost[:, 512 * dh : 512 * (dh + 1)], in0=XE[(g, j)][:, 512 * dh : 512 * (dh + 1)],
+                scalar=sb[:, 4 * g + j : 4 * g + j + 1], in1=PS[("o0", g, i)][:], op0=ALU.mult, op1=ALU.add,
+            )
+            if dh == 1:
+                nc.sync.dma_start(out=o0_v[g][:, j, :], in_=ost[:])
+                if j + 2 < 4:
+                    load_xe(g, j + 2)
+
+        with tc.tile_pool(name="prep", bufs=2) as prep:
+            RAW = {}
+
+            def load_raw(key, src):
+                RAW[key] = prep.tile([P, 4, D], BF16, name="raw", bufs=2)
+                nc.sync.dma_start(out=RAW[key][:], in_=src)
+
+            def prep_copy(key):
+                grps = []
+                for dh in range(2):
+                    grp = prep.tile([P, 512, 4], BF16, name="pgrp", bufs=2, align_bytes=64)
+                    nc.vector.tensor_copy(
+                        out=grp[:], in_=RAW[key][:, :, 512 * dh : 512 * (dh + 1)].rearrange("p j d -> p d j")
+                    )
+                    grps.append(grp)
+                return grps
+
+            def prep_quant(grps, codes, scales):
+                for dh in range(2):
+                    nc.vector.quantize_mx(
+                        out=codes[:, 512 * dh : 512 * (dh + 1)].bitcast(E4), scales=scales[:, 512 * dh : 512 * (dh + 1)],
+                        in_=grps[dh][:].rearrange("p d j -> p (d j)"),
+                    )
+
+            def x_squares(g):
+                for j in range(4):
+                    xj = prep.tile([P, D], BF16, name="xj", bufs=1)
+                    nc.vector.scalar_tensor_tensor(
+                        out=xj[:], in0=RAW[("x", g)][:, j, :], scalar=1.0, in1=RAW[("x", g)][:, j, :],
+                        op0=ALU.mult, op1=ALU.mult, accum_out=xs[:, 4 * g + j : 4 * g + j + 1],
+                    )
+
+            load_a(0, 0)
+            load_a(0, 1)
+            load_raw(("x", 0), x_v[0])
+            load_a(0, 2)
+            load_a(0, 3)
+            load_raw(("x", 1), x_v[1])
+            for m in range(4):
+                load_zt(0, m)
+            nc.sync.dma_start(out=r_bc[:], in_=r.rearrange("o one -> (o one)").partition_broadcast(P))
+            for k in range(4):
+                load_vg(0, k)
+            s_phase(0, 0)
+            s_phase(0, 1)
+            g0 = prep_copy(("x", 0))
+            u_op(0, 0)
+            u_op(0, 1)
+            s_phase(0, 2)
+            s_phase(0, 3)
+            zn_squares(0)
+            zn_sqrt(0)
+            x_squares(0)
+            prep_quant(g0, x_codes[:, 0, :], x_scales[:, 0, :])
+            load_raw(("z", 0), zq_v[0])
+            u_op(0, 2)
+            u_op(0, 3)
+            for k in range(4):
+                r_phase(0, k)
+            for k in range(4):
+                l_phase(0, k)
+            e_r(0)
+            e_phase(0, 0)
+            e_phase(0, 1)
+            sign_phase(0, 0)
+            sign_phase(0, 1)
+            g1 = prep_copy(("x", 1))
+            x_squares(1)
+            prep_quant(g1, x_codes[:, 1, :], x_scales[:, 1, :])
+            load_raw(("z", 1), zq_v[1])
+            for c in range(NG):
+                g0 = prep_copy(("z", c))
+                if c + 2 < NG:
+                    load_raw(("z", c + 2), zq_v[c + 2])
+                prep_quant(g0, z_codes[:, c, :], z_scales[:, c, :])
+            load_a(1, 0)
+            load_a(1, 1)
+
+        late = ctx.enter_context(tc.tile_pool(name="late", bufs=2))
+        bc0 = cz_pe(0)
+        cz_dve1(0)
+        mn0 = cz_pe2(0)
+        cz_dve2(0, bc0, mn0)
+
+        TZ = {}
+        LAST = 2 * NG - 1
+        AHEAD = 3
+        for hh in range(2 * NG):
+            c, h = hh // 2, hh % 2
+            nx = c + 1
+            more = nx < NG
+            pc, ph = (hh - 1) // 2, (hh - 1) % 2
+            if h == 0 and c >= 1:
+                wpe, wdve = (lambda i: out1_pe(c - 1, i)), (lambda i: out1_dve(c - 1, i))
+                weave = 8
+            elif hh == LAST:
+                wpe, wdve = (lambda i: out0_pe(0, i)), (lambda i: out0_dve(0, i))
+                weave = 8
+            else:
+                wpe, wdve = None, None
+                weave = 0
+            for i in range(min(AHEAD, weave)):
+                wpe(i)
+            chain_pair(c, h, 0, 3, None)
+            if h == 0:
+                e_phase(c, 2)
+                e_phase(c, 3)
+            if hh == 0:
+                nc.scalar.activation(out=beta[:], in_=xs[:], func=ACT.Sqrt, bias=one_c[:])
+                for k in range(4):
+                    fill_beta(0, k)
+                fill_beta(1, 0)
+                fill_beta(1, 1)
+            if hh >= 1:
+                post_sums(pc, ph)
+                if h == 0:
+                    TZ[pc] = fin_small(pc)
+            pe_diag(c, h)
+            if more and h == 0:
+                s_phase(nx, 0)
+                s_phase(nx, 1)
+                load_a(nx, 2)
+                load_a(nx, 3)
+                fill_beta(nx, 2)
+                fill_beta(nx, 3)
+            if more and h == 1:
+                u_op(nx, 2)
+                u_op(nx, 3)
+                for k in range(4):
+                    r_phase(nx, k)
+                if nx + 1 < NG:
+                    load_a(nx + 1, 0)
+                    load_a(nx + 1, 1)
+                    fill_beta(nx + 1, 0)
+                    fill_beta(nx + 1, 1)
+
+            def woven(t):
+                if t < weave:
+                    wdve(t)
+                    if t + AHEAD < weave:
+                        wpe(t + AHEAD)
+
+            chain_pair(c, h, 3, 8, woven)
+            if hh == LAST:
+                pe_transposes(c, h)
+                pe_minis(c, h)
+            else:
+                pe_minis(c, h)
+                if hh >= 1:
+                    evac(pc, ph)
+                pe_transposes(c, h)
+            if hh == 0:
+                nc.vector.reciprocal(out=rbeta[:], in_=beta[:])
+            if h == 0:
+                sign_phase(c, 2)
+                sign_phase(c, 3)
+            if more and h == 0:
+                load_vg(nx, 0)
+                load_vg(nx, 1)
+                for m in range(4):
+                    load_zt(nx, m)
+                u_op(nx, 0)
+                u_op(nx, 1)
+                s_phase(nx, 2)
+                s_phase(nx, 3)
+                zn_squares(nx)
+                zn_sqrt(nx)
+            if more and h == 1:
+                for k in range(4):
+                    l_phase(nx, k)
+                load_vg(nx, 2)
+                load_vg(nx, 3)
+                e_r(nx)
+                e_phase(nx, 0)
+                e_phase(nx, 1)
+                sign_phase(nx, 0)
+                sign_phase(nx, 1)
+            di = post_tk(c, h)
+            if hh >= 1 and hh != LAST:
+                post_ft_q(pc, ph)
+            post_tk_q(c, h, di)
+            if h == 1:
+                if more:
+                    bcn = cz_pe(nx)
+                    cz_dve1(nx)
+                    mnn = cz_pe2(nx)
+                    cz_dve2(nx, bcn, mnn)
+                for m in range(4):
+                    load_zt(c, m)
+            if hh == LAST - 1:
+                load_xe(0, 0)
+                load_xe(0, 1)
+                evac(c, h)
+                post_ft_q(c, h)
+                out0_scale(0)
+        load_xe(1, 0)
+        load_xe(1, 1)
+        evac(NG - 1, 1)
+        post_ft_q(NG - 1, 1)
+        out0_scale(1)
+        for i in range(AHEAD):
+            out0_pe(1, i)
+        post_sums(NG - 1, 1)
+        TZ[NG - 1] = fin_small(NG - 1)
+        for i in range(16):
+            if i < 8:
+                out0_dve(1, i)
+            else:
+                out1_dve(NG - 1, i - 8)
+            n = i + AHEAD
+            if n < 8:
+                out0_pe(1, n)
+            elif n < 16:
+                out1_pe(NG - 1, n - 8)

@@ -43,6 +43,8 @@ def tile_pvfc_v_kernel(tc, x, z, r, bias, arg, v, grad_out, out_0, out_1):
         make_identity(nc, ident[:])
         one_c = keep.tile([P, 1], F32, name="one_c")
         nc.vector.memset(one_c[:], 1.0)
+        warm = keep.tile([P, 1], F32, name="warm")
+        nc.scalar.activation(out=warm[:], in_=one_c[:], func=ACT.Sqrt)
 
         x_codes = keep.tile([P, 2, D], U32, name="x_codes", align_bytes=64)
         x_scales = keep.tile([P, 2, D], U8, name="x_scales", align_bytes=64)
@@ -136,7 +138,7 @@ def tile_pvfc_v_kernel(tc, x, z, r, bias, arg, v, grad_out, out_0, out_1):
             nc.scalar.activation(out=V[(c, k)][:], in_=V[(c, k)][:], func=ACT.Exp)
 
         def sign_phase(c, k):
-            SG[(c, k)] = strm.tile([P, 2, CH], BF16, name="SG", bufs=2)
+            SG[(c, k)] = strm.tile([P, 2, CH], BF16, name="SG", bufs=4)
             nc.scalar.activation(out=blocks(SG[(c, k)]), in_=A[(c, k)][:, :, :, 0:P], func=ACT.Sign)
 
         def cz_pe(c):
@@ -152,12 +154,10 @@ def tile_pvfc_v_kernel(tc, x, z, r, bias, arg, v, grad_out, out_0, out_1):
             return bc
 
         def cz_dve1(c):
-            CHALF[c] = strm.tile([P, CH], F32, name="CHALF", bufs=2)
+            CHALF[c] = strm.tile([P, CH], F32, name="CHALF", bufs=1)
             SHH[c] = strm.tile([P, CH], F32, name="SHH", bufs=1)
             nc.vector.tensor_tensor(out=CHALF[c][:], in0=ER[(c, 0)][:], in1=ER[(c, 1)][:], op=ALU.add)
             nc.vector.tensor_tensor(out=SHH[c][:], in0=ER[(c, 1)][:], in1=ER[(c, 0)][:], op=ALU.subtract)
-            nc.vector.tensor_scalar(out=CHALF[c][:], in0=CHALF[c][:], scalar1=0.5, scalar2=None, op0=ALU.mult)
-            nc.vector.tensor_scalar(out=SHH[c][:], in0=SHH[c][:], scalar1=0.5, scalar2=None, op0=ALU.mult)
             nc.vector.reciprocal(out=rzn[:, 4 * c : 4 * c + 4], in_=zn[:, 4 * c : 4 * c + 4])
 
         def cz_pe2(c):
@@ -168,9 +168,11 @@ def tile_pvfc_v_kernel(tc, x, z, r, bias, arg, v, grad_out, out_0, out_1):
                 )
             return mn
 
-        def cz_dve2(c, bc, mn):
-            ZSN[c] = strm.tile([P, CH], F32, name="ZSN", bufs=2)
+        def cz_dve2(c, bc):
+            ZSN[c] = strm.tile([P, CH], F32, name="ZSN", bufs=1)
             nc.vector.tensor_tensor(out=ZSN[c][:], in0=bc[:], in1=SHH[c][:], op=ALU.mult)
+
+        def cz_dve3(c, mn):
             nc.vector.tensor_copy(out=shn[:, 4 * c : 4 * c + 4], in_=mn[:, 0:4])
 
         def chain_steps(c, k):
@@ -189,7 +191,7 @@ def tile_pvfc_v_kernel(tc, x, z, r, bias, arg, v, grad_out, out_0, out_1):
             return [
                 lambda: nc.vector.tensor_tensor(out=vv[:], in0=vv[:], in1=e2[:], op=ALU.add),
                 lambda: nc.vector.scalar_tensor_tensor(
-                    out=vv[:], in0=vv[:], scalar=0.5, in1=g2[:], op0=ALU.mult, op1=ALU.mult
+                    out=vv[:], in0=vv[:], scalar=0.25, in1=g2[:], op0=ALU.mult, op1=ALU.mult
                 ),
                 lambda: nc.vector.tensor_tensor(out=q[:], in0=vv[:], in1=q[:], op=ALU.mult),
                 lambda: nc.vector.tensor_tensor(
@@ -235,7 +237,8 @@ def tile_pvfc_v_kernel(tc, x, z, r, bias, arg, v, grad_out, out_0, out_1):
             for m in range(4):
                 blk = slice(P * m, P * (m + 1))
                 if m % 2 == 0:
-                    DG[(c, h, m // 2)] = psum.tile([P, 2, AW], F32, name="dg", bufs=2)
+                    dgt = psum.tile([P, 512], F32, name="dg", bufs=2)
+                    DG[(c, h, m // 2)] = dgt[:, 0 : 2 * AW].rearrange("p (m w) -> p m w", m=2)
                 for j in range(4):
                     k = 2 * h + j // 2
                     nc.tensor.matmul(
@@ -284,6 +287,8 @@ def tile_pvfc_v_kernel(tc, x, z, r, bias, arg, v, grad_out, out_0, out_1):
                 nc.vector.tensor_copy(
                     out=sums[:, 2 * c + h, 4 + 2 * mp : 6 + 2 * mp], in_=DG[(c, h, mp)][:, :, P : P + 1].rearrange("p m one -> p (m one)")
                 )
+
+        def post_mini(c, h):
             nc.vector.tensor_copy(out=sums[:, 2 * c + h, 0:4], in_=MINI[(c, h)][:, 0:4])
 
         def fin_small(c):
@@ -294,15 +299,30 @@ def tile_pvfc_v_kernel(tc, x, z, r, bias, arg, v, grad_out, out_0, out_1):
             nc.gpsimd.tensor_tensor(out=s12[:], in0=sums[:, 2 * c, :], in1=sums[:, 2 * c + 1, :], op=ALU.add)
             nc.gpsimd.tensor_tensor(out=ta[:], in0=s12[:, 0:4], in1=s12[:, 8:12], op=ALU.subtract)
             nc.gpsimd.tensor_tensor(out=tb[:], in0=s12[:, 4:8], in1=shn[:, 4 * c : 4 * c + 4], op=ALU.mult)
+            nc.gpsimd.tensor_tensor(out=ta[:], in0=ta[:], in1=ta[:], op=ALU.add)
             nc.gpsimd.tensor_tensor(out=ta[:], in0=ta[:], in1=tb[:], op=ALU.add)
             nc.gpsimd.tensor_tensor(out=tz[:], in0=ta[:], in1=rzn[:, 4 * c : 4 * c + 4], op=ALU.mult)
             return tz
 
         PS, OST, XE = {}, {}, {}
+        TAIL = []
+
+        def acc_tile():
+            if len(TAIL) == 0:
+                return psum.tile([P, 512], F32, name="mx", bufs=3)
+            which = (len(TAIL) - 1) % 7
+            TAIL.append(0)
+            if which < 3:
+                return psum.tile([P, 512], F32, name="mx", bufs=3)
+            if which < 5:
+                tpt = psum.tile([P, 4, P], F32, name="tp", bufs=2)
+                return tpt[:].rearrange("p a b -> p (a b)")
+            return psum.tile([P, 512], F32, name="dg", bufs=2)
+
 
         def out1_pe(c, i):
             m, dh = i // 2, i % 2
-            PS[("o1", c, i)] = psum.tile([P, 512], F32, name="mx", bufs=3)
+            PS[("o1", c, i)] = acc_tile()
             for g in range(2):
                 nc.tensor.matmul_mx(
                     out=PS[("o1", c, i)][:],
@@ -336,7 +356,7 @@ def tile_pvfc_v_kernel(tc, x, z, r, bias, arg, v, grad_out, out_0, out_1):
 
         def out0_pe(g, i):
             s, dh = 4 * g + i // 2, i % 2
-            PS[("o0", g, i)] = psum.tile([P, 512], F32, name="mx", bufs=3)
+            PS[("o0", g, i)] = acc_tile()
             for c in range(NG):
                 nc.tensor.matmul_mx(
                     out=PS[("o0", g, i)][:],
@@ -411,9 +431,12 @@ def tile_pvfc_v_kernel(tc, x, z, r, bias, arg, v, grad_out, out_0, out_1):
             u_op(0, 1)
             s_phase(0, 2)
             s_phase(0, 3)
+            x_squares(0)
             zn_squares(0)
             zn_sqrt(0)
-            x_squares(0)
+            nc.scalar.activation(out=beta[:, 0:4], in_=xs[:, 0:4], func=ACT.Sqrt, bias=one_c[:])
+            fill_beta(0, 0)
+            fill_beta(0, 1)
             prep_quant(g0, x_codes[:, 0, :], x_scales[:, 0, :])
             load_raw(("z", 0), zq_v[0])
             u_op(0, 2)
@@ -443,7 +466,8 @@ def tile_pvfc_v_kernel(tc, x, z, r, bias, arg, v, grad_out, out_0, out_1):
         bc0 = cz_pe(0)
         cz_dve1(0)
         mn0 = cz_pe2(0)
-        cz_dve2(0, bc0, mn0)
+        cz_dve2(0, bc0)
+        cz_dve3(0, mn0)
 
         TZ = {}
         LAST = 2 * NG - 1
@@ -462,23 +486,36 @@ def tile_pvfc_v_kernel(tc, x, z, r, bias, arg, v, grad_out, out_0, out_1):
             else:
                 wpe, wdve = None, None
                 weave = 0
+
+            def woven(t):
+                if t < weave:
+                    wdve(t)
+                    if t + AHEAD < weave:
+                        wpe(t + AHEAD)
+
             for i in range(min(AHEAD, weave)):
                 wpe(i)
+            if hh >= 1:
+                post_sums(pc, ph)
             chain_pair(c, h, 0, 3, None)
             if h == 0:
                 e_phase(c, 2)
                 e_phase(c, 3)
+                sign_phase(c, 2)
+                sign_phase(c, 3)
+                if more:
+                    e_r(nx)
             if hh == 0:
-                nc.scalar.activation(out=beta[:], in_=xs[:], func=ACT.Sqrt, bias=one_c[:])
-                for k in range(4):
-                    fill_beta(0, k)
+                nc.scalar.activation(out=beta[:, 4:8], in_=xs[:, 4:8], func=ACT.Sqrt, bias=one_c[:])
+                fill_beta(0, 2)
+                fill_beta(0, 3)
                 fill_beta(1, 0)
                 fill_beta(1, 1)
+            pe_diag(c, h)
             if hh >= 1:
-                post_sums(pc, ph)
+                post_mini(pc, ph)
                 if h == 0:
                     TZ[pc] = fin_small(pc)
-            pe_diag(c, h)
             if more and h == 0:
                 s_phase(nx, 0)
                 s_phase(nx, 1)
@@ -489,6 +526,7 @@ def tile_pvfc_v_kernel(tc, x, z, r, bias, arg, v, grad_out, out_0, out_1):
             if more and h == 1:
                 u_op(nx, 2)
                 u_op(nx, 3)
+                bcn = cz_pe(nx)
                 for k in range(4):
                     r_phase(nx, k)
                 if nx + 1 < NG:
@@ -496,27 +534,20 @@ def tile_pvfc_v_kernel(tc, x, z, r, bias, arg, v, grad_out, out_0, out_1):
                     load_a(nx + 1, 1)
                     fill_beta(nx + 1, 0)
                     fill_beta(nx + 1, 1)
-
-            def woven(t):
-                if t < weave:
-                    wdve(t)
-                    if t + AHEAD < weave:
-                        wpe(t + AHEAD)
-
-            chain_pair(c, h, 3, 8, woven)
             if hh == LAST:
+                chain_pair(c, h, 3, 4, woven)
                 pe_transposes(c, h)
+                evac(c, h)
+                chain_pair(c, h, 4, 8, lambda t: woven(t + 2))
                 pe_minis(c, h)
             else:
+                chain_pair(c, h, 3, 8, woven)
                 pe_minis(c, h)
                 if hh >= 1:
                     evac(pc, ph)
                 pe_transposes(c, h)
             if hh == 0:
                 nc.vector.reciprocal(out=rbeta[:], in_=beta[:])
-            if h == 0:
-                sign_phase(c, 2)
-                sign_phase(c, 3)
             if more and h == 0:
                 load_vg(nx, 0)
                 load_vg(nx, 1)
@@ -533,7 +564,6 @@ def tile_pvfc_v_kernel(tc, x, z, r, bias, arg, v, grad_out, out_0, out_1):
                     l_phase(nx, k)
                 load_vg(nx, 2)
                 load_vg(nx, 3)
-                e_r(nx)
                 e_phase(nx, 0)
                 e_phase(nx, 1)
                 sign_phase(nx, 0)
@@ -544,10 +574,10 @@ def tile_pvfc_v_kernel(tc, x, z, r, bias, arg, v, grad_out, out_0, out_1):
             post_tk_q(c, h, di)
             if h == 1:
                 if more:
-                    bcn = cz_pe(nx)
                     cz_dve1(nx)
+                    cz_dve2(nx, bcn)
                     mnn = cz_pe2(nx)
-                    cz_dve2(nx, bcn, mnn)
+                    cz_dve3(nx, mnn)
                 for m in range(4):
                     load_zt(c, m)
             if hh == LAST - 1:
@@ -558,19 +588,21 @@ def tile_pvfc_v_kernel(tc, x, z, r, bias, arg, v, grad_out, out_0, out_1):
                 out0_scale(0)
         load_xe(1, 0)
         load_xe(1, 1)
-        evac(NG - 1, 1)
         post_ft_q(NG - 1, 1)
         out0_scale(1)
-        for i in range(AHEAD):
-            out0_pe(1, i)
         post_sums(NG - 1, 1)
+        post_mini(NG - 1, 1)
         TZ[NG - 1] = fin_small(NG - 1)
+        TAIL.append(0)
+        DEEP = 7
+        for i in range(DEEP):
+            out0_pe(1, i)
         for i in range(16):
             if i < 8:
                 out0_dve(1, i)
             else:
                 out1_dve(NG - 1, i - 8)
-            n = i + AHEAD
+            n = i + DEEP
             if n < 8:
                 out0_pe(1, n)
             elif n < 16:

@@ -55,6 +55,7 @@ def tile_pvfc_v_kernel(tc, x, z, r, bias, arg, v, grad_out, out_0, out_1):
         r_bc = keep.tile([P, OUT], BF16, name="r_bc")
 
         xs = keep.tile([P, 8], F32, name="xs")
+        xs2 = keep.tile([P, 4], F32, name="xs2")
         beta = keep.tile([P, 8], F32, name="beta")
         rbeta = keep.tile([P, 8], F32, name="rbeta")
         zs2 = keep.tile([P, 4 * NG], F32, name="zs2")
@@ -62,7 +63,8 @@ def tile_pvfc_v_kernel(tc, x, z, r, bias, arg, v, grad_out, out_0, out_1):
         rzn = keep.tile([P, 4 * NG], F32, name="rzn")
         shn = keep.tile([P, 4 * NG], F32, name="shn")
         dbp = keep.tile([P, 8, NG], F32, name="dbp")
-        sums = keep.tile([P, 2 * NG, 12], F32, name="sums")
+        sums_a = keep.tile([P, 2 * NG, 8], F32, name="sums_a")
+        sums_d = keep.tile([P, 2 * NG, 8], F32, name="sums_d")
         sb = keep.tile([P, 8], F32, name="sb")
 
         A, V, GT, Q, M, WT, E2, SG = {}, {}, {}, {}, {}, {}, {}, {}
@@ -104,17 +106,16 @@ def tile_pvfc_v_kernel(tc, x, z, r, bias, arg, v, grad_out, out_0, out_1):
             WT[(c, k)] = strm.tile([P, 2, CH], F32, name="WT", bufs=2)
             M[(c, k)] = strm.tile([P, 2, CH], F32, name="M", bufs=6)
             nc.scalar.activation(out=blocks(Q[(c, k)]), in_=A[(c, k)][:, :, :, 0:P], func=ACT.Square)
-            nc.scalar.activation(out=WT[(c, k)][:], in_=Q[(c, k)][:], func=ACT.Sqrt, bias=one_c[:])
             nc.scalar.activation(out=blocks(M[(c, k)]), in_=A[(c, k)][:, :, :, 0:P], func=ACT.Abs)
+            nc.scalar.activation(out=WT[(c, k)][:], in_=Q[(c, k)][:], func=ACT.Sqrt, bias=one_c[:])
 
         def u_op(c, k):
             nc.vector.tensor_tensor(out=M[(c, k)][:], in0=M[(c, k)][:], in1=WT[(c, k)][:], op=ALU.add)
 
         def zn_squares(c):
             for m in range(4):
-                sq = strm.tile([P, D], BF16, name="sq", bufs=1)
                 nc.scalar.activation(
-                    out=sq[:], in_=ZT[(c, m)][:], func=ACT.Square, accum_out=zs2[:, 4 * c + m : 4 * c + m + 1]
+                    out=ZT[(c, m)][:], in_=ZT[(c, m)][:], func=ACT.Square, accum_out=zs2[:, 4 * c + m : 4 * c + m + 1]
                 )
 
         def zn_sqrt(c):
@@ -132,10 +133,12 @@ def tile_pvfc_v_kernel(tc, x, z, r, bias, arg, v, grad_out, out_0, out_1):
             nc.scalar.activation(out=ER[(c, 0)][:], in_=r_bc[:, cols(c)], func=ACT.Exp)
             nc.scalar.activation(out=ER[(c, 1)][:], in_=r_bc[:, cols(c)], func=ACT.Exp, scale=-1.0)
 
-        def e_phase(c, k):
-            E2[(c, k)] = strm.tile([P, 2, CH], F32, name="E2", bufs=2)
-            nc.scalar.activation(out=E2[(c, k)][:], in_=V[(c, k)][:], func=ACT.Exp, scale=-1.0)
-            nc.scalar.activation(out=V[(c, k)][:], in_=V[(c, k)][:], func=ACT.Exp)
+        def e_phase(c, h):
+            for k in (2 * h, 2 * h + 1):
+                E2[(c, k)] = strm.tile([P, 2, CH], F32, name="E2", bufs=2)
+                nc.scalar.activation(out=E2[(c, k)][:], in_=V[(c, k)][:], func=ACT.Exp, scale=-1.0)
+            for k in (2 * h, 2 * h + 1):
+                nc.scalar.activation(out=V[(c, k)][:], in_=V[(c, k)][:], func=ACT.Exp)
 
         def sign_phase(c, k):
             SG[(c, k)] = strm.tile([P, 2, CH], BF16, name="SG", bufs=4)
@@ -173,7 +176,7 @@ def tile_pvfc_v_kernel(tc, x, z, r, bias, arg, v, grad_out, out_0, out_1):
             nc.vector.tensor_tensor(out=ZSN[c][:], in0=bc[:], in1=SHH[c][:], op=ALU.mult)
 
         def cz_dve3(c, mn):
-            nc.vector.tensor_copy(out=shn[:, 4 * c : 4 * c + 4], in_=mn[:, 0:4])
+            nc.scalar.copy(out=shn[:, 4 * c : 4 * c + 4], in_=mn[:, 0:4])
 
         def chain_steps(c, k):
             sg, vv, g2, q, mm, e2 = SG[(c, k)], V[(c, k)], GT[(c, k)], Q[(c, k)], M[(c, k)], E2[(c, k)]
@@ -181,7 +184,7 @@ def tile_pvfc_v_kernel(tc, x, z, r, bias, arg, v, grad_out, out_0, out_1):
             d16 = D16[(c, h)]
 
             def dbeta_step(jj):
-                junk = late.tile([P, CH], BF16, name="junk", bufs=1)
+                junk = late.tile([P, CH], BF16, name="junk", bufs=2)
                 s = 4 * h + 2 * jp + jj
                 nc.vector.scalar_tensor_tensor(
                     out=junk[:], in0=q[:, jj, :], scalar=1.0, in1=ZSN[c][:], op0=ALU.mult, op1=ALU.mult,
@@ -278,27 +281,30 @@ def tile_pvfc_v_kernel(tc, x, z, r, bias, arg, v, grad_out, out_0, out_1):
 
         def post_sums(c, h):
             for m in range(4):
-                jk = late.tile([P, P], F32, name="jk", bufs=1)
+                jk = late.tile([P, P], F32, name="jk", bufs=4)
                 nc.vector.scalar_tensor_tensor(
                     out=jk[:], in0=DG[(c, h, m // 2)][:, m % 2, 0:P], scalar=1.0, in1=ident[:], op0=ALU.mult,
-                    op1=ALU.mult, accum_out=sums[:, 2 * c + h, 8 + m : 9 + m],
+                    op1=ALU.mult, accum_out=sums_d[:, 2 * c + h, m : m + 1],
                 )
             for mp in range(2):
-                nc.vector.tensor_copy(
-                    out=sums[:, 2 * c + h, 4 + 2 * mp : 6 + 2 * mp], in_=DG[(c, h, mp)][:, :, P : P + 1].rearrange("p m one -> p (m one)")
+                nc.scalar.copy(
+                    out=sums_a[:, 2 * c + h, 4 + 2 * mp : 6 + 2 * mp],
+                    in_=DG[(c, h, mp)][:, :, P : P + 1].rearrange("p m one -> p (m one)"),
                 )
 
         def post_mini(c, h):
-            nc.vector.tensor_copy(out=sums[:, 2 * c + h, 0:4], in_=MINI[(c, h)][:, 0:4])
+            nc.scalar.copy(out=sums_a[:, 2 * c + h, 0:4], in_=MINI[(c, h)][:, 0:4])
 
         def fin_small(c):
-            s12 = keep.tile([P, 12], F32, name="s12", bufs=2)
+            s8 = keep.tile([P, 8], F32, name="s8", bufs=2)
+            t2 = keep.tile([P, 4], F32, name="t2", bufs=2)
             ta = keep.tile([P, 4], F32, name="ta", bufs=2)
             tb = keep.tile([P, 4], F32, name="tb", bufs=2)
             tz = keep.tile([P, 4], F32, name="tz", bufs=2)
-            nc.gpsimd.tensor_tensor(out=s12[:], in0=sums[:, 2 * c, :], in1=sums[:, 2 * c + 1, :], op=ALU.add)
-            nc.gpsimd.tensor_tensor(out=ta[:], in0=s12[:, 0:4], in1=s12[:, 8:12], op=ALU.subtract)
-            nc.gpsimd.tensor_tensor(out=tb[:], in0=s12[:, 4:8], in1=shn[:, 4 * c : 4 * c + 4], op=ALU.mult)
+            nc.gpsimd.tensor_tensor(out=s8[:], in0=sums_a[:, 2 * c, :], in1=sums_a[:, 2 * c + 1, :], op=ALU.add)
+            nc.gpsimd.tensor_tensor(out=t2[:], in0=sums_d[:, 2 * c, 0:4], in1=sums_d[:, 2 * c + 1, 0:4], op=ALU.add)
+            nc.gpsimd.tensor_tensor(out=ta[:], in0=s8[:, 0:4], in1=t2[:], op=ALU.subtract)
+            nc.gpsimd.tensor_tensor(out=tb[:], in0=s8[:, 4:8], in1=shn[:, 4 * c : 4 * c + 4], op=ALU.mult)
             nc.gpsimd.tensor_tensor(out=ta[:], in0=ta[:], in1=ta[:], op=ALU.add)
             nc.gpsimd.tensor_tensor(out=ta[:], in0=ta[:], in1=tb[:], op=ALU.add)
             nc.gpsimd.tensor_tensor(out=tz[:], in0=ta[:], in1=rzn[:, 4 * c : 4 * c + 4], op=ALU.mult)
@@ -320,6 +326,12 @@ def tile_pvfc_v_kernel(tc, x, z, r, bias, arg, v, grad_out, out_0, out_1):
             return psum.tile([P, 512], F32, name="dg", bufs=2)
 
 
+        def ost_tile():
+            if len(TAIL) == 0:
+                return late.tile([P, D], F32, name="ost", bufs=2)
+            qt = strm.tile([P, 2, CH], F32, name="Q", bufs=6)
+            return qt[:].rearrange("p a b -> p (a b)")
+
         def out1_pe(c, i):
             m, dh = i // 2, i % 2
             PS[("o1", c, i)] = acc_tile()
@@ -336,7 +348,7 @@ def tile_pvfc_v_kernel(tc, x, z, r, bias, arg, v, grad_out, out_0, out_1):
         def out1_dve(c, i):
             m, dh = i // 2, i % 2
             if dh == 0:
-                OST[("o1", c, m)] = late.tile([P, D], F32, name="ost", bufs=2)
+                OST[("o1", c, m)] = ost_tile()
             ost = OST[("o1", c, m)]
             nc.vector.scalar_tensor_tensor(
                 out=ost[:, 512 * dh : 512 * (dh + 1)], in0=ZT[(c, m)][:, 512 * dh : 512 * (dh + 1)],
@@ -370,7 +382,7 @@ def tile_pvfc_v_kernel(tc, x, z, r, bias, arg, v, grad_out, out_0, out_1):
         def out0_dve(g, i):
             j, dh = i // 2, i % 2
             if dh == 0:
-                OST[("o0", g, j)] = late.tile([P, D], F32, name="ost", bufs=2)
+                OST[("o0", g, j)] = ost_tile()
             ost = OST[("o0", g, j)]
             nc.vector.scalar_tensor_tensor(
                 out=ost[:, 512 * dh : 512 * (dh + 1)], in0=XE[(g, j)][:, 512 * dh : 512 * (dh + 1)],
@@ -407,7 +419,7 @@ def tile_pvfc_v_kernel(tc, x, z, r, bias, arg, v, grad_out, out_0, out_1):
 
             def x_squares(g):
                 for j in range(4):
-                    xj = prep.tile([P, D], BF16, name="xj", bufs=1)
+                    xj = prep.tile([P, D], BF16, name="xj", bufs=2)
                     nc.vector.scalar_tensor_tensor(
                         out=xj[:], in0=RAW[("x", g)][:, j, :], scalar=1.0, in1=RAW[("x", g)][:, j, :],
                         op0=ALU.mult, op1=ALU.mult, accum_out=xs[:, 4 * g + j : 4 * g + j + 1],
@@ -447,11 +459,13 @@ def tile_pvfc_v_kernel(tc, x, z, r, bias, arg, v, grad_out, out_0, out_1):
                 l_phase(0, k)
             e_r(0)
             e_phase(0, 0)
-            e_phase(0, 1)
             sign_phase(0, 0)
             sign_phase(0, 1)
+            for j in range(4):
+                xt = strm.tile([P, D], BF16, name="ZT", bufs=4)
+                nc.sync.dma_start(out=xt[:], in_=x_v[1][:, j, :])
+                nc.scalar.activation(out=xt[:], in_=xt[:], func=ACT.Square, accum_out=xs2[:, j : j + 1])
             g1 = prep_copy(("x", 1))
-            x_squares(1)
             prep_quant(g1, x_codes[:, 1, :], x_scales[:, 1, :])
             load_raw(("z", 1), zq_v[1])
             for c in range(NG):
@@ -469,7 +483,7 @@ def tile_pvfc_v_kernel(tc, x, z, r, bias, arg, v, grad_out, out_0, out_1):
         cz_dve2(0, bc0)
         cz_dve3(0, mn0)
 
-        TZ = {}
+        TZ, MN = {}, {}
         LAST = 2 * NG - 1
         AHEAD = 3
         for hh in range(2 * NG):
@@ -488,34 +502,37 @@ def tile_pvfc_v_kernel(tc, x, z, r, bias, arg, v, grad_out, out_0, out_1):
                 weave = 0
 
             def woven(t):
-                if t < weave:
-                    wdve(t)
-                    if t + AHEAD < weave:
-                        wpe(t + AHEAD)
+                i = t if t < AHEAD else t - 2
+                if i < weave and t != AHEAD and t != AHEAD + 1:
+                    wdve(i)
+                    if i + AHEAD < weave:
+                        wpe(i + AHEAD)
 
-            for i in range(min(AHEAD, weave)):
-                wpe(i)
             if hh >= 1:
                 post_sums(pc, ph)
-            chain_pair(c, h, 0, 3, None)
+                if h == 0:
+                    cz_dve3(c, MN[c])
+            for i in range(min(AHEAD, weave)):
+                wpe(i)
+            chain_pair(c, h, 0, 1, None)
+            if hh >= 1:
+                post_mini(pc, ph)
+                if h == 0:
+                    TZ[pc] = fin_small(pc)
+            chain_pair(c, h, 1, 3, None)
             if h == 0:
-                e_phase(c, 2)
-                e_phase(c, 3)
+                e_phase(c, 1)
                 sign_phase(c, 2)
                 sign_phase(c, 3)
                 if more:
                     e_r(nx)
             if hh == 0:
-                nc.scalar.activation(out=beta[:, 4:8], in_=xs[:, 4:8], func=ACT.Sqrt, bias=one_c[:])
+                nc.scalar.activation(out=beta[:, 4:8], in_=xs2[:], func=ACT.Sqrt, bias=one_c[:])
                 fill_beta(0, 2)
                 fill_beta(0, 3)
                 fill_beta(1, 0)
                 fill_beta(1, 1)
             pe_diag(c, h)
-            if hh >= 1:
-                post_mini(pc, ph)
-                if h == 0:
-                    TZ[pc] = fin_small(pc)
             if more and h == 0:
                 s_phase(nx, 0)
                 s_phase(nx, 1)
@@ -565,7 +582,6 @@ def tile_pvfc_v_kernel(tc, x, z, r, bias, arg, v, grad_out, out_0, out_1):
                 load_vg(nx, 2)
                 load_vg(nx, 3)
                 e_phase(nx, 0)
-                e_phase(nx, 1)
                 sign_phase(nx, 0)
                 sign_phase(nx, 1)
             di = post_tk(c, h)
@@ -576,8 +592,7 @@ def tile_pvfc_v_kernel(tc, x, z, r, bias, arg, v, grad_out, out_0, out_1):
                 if more:
                     cz_dve1(nx)
                     cz_dve2(nx, bcn)
-                    mnn = cz_pe2(nx)
-                    cz_dve3(nx, mnn)
+                    MN[nx] = cz_pe2(nx)
                 for m in range(4):
                     load_zt(c, m)
             if hh == LAST - 1:

@@ -10,16 +10,19 @@ F32 = mybir.dt.float32
 BF16 = mybir.dt.bfloat16
 U32 = mybir.dt.uint32
 U8 = mybir.dt.uint8
-E4 = mybir.dt.float8_e4m3fn_x4
-E5 = mybir.dt.float8_e5m2_x4
+E4M3 = mybir.dt.float8_e4m3fn_x4
+E5M2 = mybir.dt.float8_e5m2_x4
 ALU = mybir.AluOpType
 ACT = mybir.ActivationFunctionType
 AX = mybir.AxisListType
 
 P = 128
 CH = 512
-NG = OUT // CH
-AW = 136
+NCH = OUT // CH
+NB = 512
+BLK = 136
+AHEAD = 3
+TAIL_BANKS = 7
 
 
 def tile_pvfc_v_kernel(tc, x, z, r, bias, arg, v, grad_out, out_0, out_1):
@@ -28,370 +31,359 @@ def tile_pvfc_v_kernel(tc, x, z, r, bias, arg, v, grad_out, out_0, out_1):
     v_v = v.rearrange("(g p j) o -> g p j o", g=2, j=4)
     go_v = grad_out.rearrange("(g p j) o -> g p j o", g=2, j=4)
     x_v = x.rearrange("(g p j) d -> g p j d", g=2, j=4)
-    o0_v = out_0.rearrange("(g p j) d -> g p j d", g=2, j=4)
-    zq_v = z.rearrange("(c p j) d -> c p j d", c=NG, j=4)
-    zn_v = z.rearrange("(c m p) d -> c p m d", c=NG, m=4)
-    o1_v = out_1.rearrange("(c m p) d -> c p m d", c=NG, m=4)
+    out0_v = out_0.rearrange("(g p j) d -> g p j d", g=2, j=4)
+    z_k = z.rearrange("(c p j) d -> c p j d", c=NCH, j=4)
+    z_rows = z.rearrange("(c m p) d -> c p m d", c=NCH, m=4)
+    out1_v = out_1.rearrange("(c m p) d -> c p m d", c=NCH, m=4)
 
     with ExitStack() as ctx:
         ctx.enter_context(tc.manual_schedule())
         keep = ctx.enter_context(tc.tile_pool(name="keep", bufs=1))
-        strm = ctx.enter_context(tc.tile_pool(name="strm", bufs=2))
+        ring = ctx.enter_context(tc.tile_pool(name="ring", bufs=2))
         psum = ctx.enter_context(tc.psum_pool(name="psum", bufs=1))
 
         ident = keep.tile([P, P], F32, name="ident")
         make_identity(nc, ident[:])
-        one_c = keep.tile([P, 1], F32, name="one_c")
-        nc.vector.memset(one_c[:], 1.0)
+        ones = keep.tile([P, 1], F32, name="ones")
+        nc.vector.memset(ones[:], 1.0)
         warm = keep.tile([P, 1], F32, name="warm")
-        nc.scalar.activation(out=warm[:], in_=one_c[:], func=ACT.Sqrt)
+        nc.scalar.activation(out=warm[:], in_=ones[:], func=ACT.Sqrt)
 
         x_codes = keep.tile([P, 2, D], U32, name="x_codes", align_bytes=64)
         x_scales = keep.tile([P, 2, D], U8, name="x_scales", align_bytes=64)
-        z_codes = keep.tile([P, NG, D], U32, name="z_codes", align_bytes=64)
-        z_scales = keep.tile([P, NG, D], U8, name="z_scales", align_bytes=64)
-        ft_codes = keep.tile([P, NG, B], U32, name="ft_codes", align_bytes=64)
-        ft_scales = keep.tile([P, NG, B], U8, name="ft_scales", align_bytes=64)
-        r_bc = keep.tile([P, OUT], BF16, name="r_bc")
+        z_codes = keep.tile([P, NCH, D], U32, name="z_codes", align_bytes=64)
+        z_scales = keep.tile([P, NCH, D], U8, name="z_scales", align_bytes=64)
+        f_codes = keep.tile([P, NCH, B], U32, name="f_codes", align_bytes=64)
+        f_scales = keep.tile([P, NCH, B], U8, name="f_scales", align_bytes=64)
+        r_rows = keep.tile([P, OUT], BF16, name="r_rows")
 
-        xs = keep.tile([P, 8], F32, name="xs")
-        xs2 = keep.tile([P, 4], F32, name="xs2")
+        xsq_v = keep.tile([P, 4], F32, name="xsq_v")
+        xsq_s = keep.tile([P, 4], F32, name="xsq_s")
         beta = keep.tile([P, 8], F32, name="beta")
         rbeta = keep.tile([P, 8], F32, name="rbeta")
-        zs2 = keep.tile([P, 4 * NG], F32, name="zs2")
-        zn = keep.tile([P, 4 * NG], F32, name="zn")
-        rzn = keep.tile([P, 4 * NG], F32, name="rzn")
-        shn = keep.tile([P, 4 * NG], F32, name="shn")
-        dbp = keep.tile([P, 8, NG], F32, name="dbp")
-        sums_a = keep.tile([P, 2 * NG, 8], F32, name="sums_a")
-        sums_d = keep.tile([P, 2 * NG, 8], F32, name="sums_d")
-        sb = keep.tile([P, 8], F32, name="sb")
+        zsq = keep.tile([P, 4 * NCH], F32, name="zsq")
+        zn = keep.tile([P, 4 * NCH], F32, name="zn")
+        rzn = keep.tile([P, 4 * NCH], F32, name="rzn")
+        sh2n = keep.tile([P, 4 * NCH], F32, name="sh2n")
+        dbeta_part = keep.tile([P, 8, NCH], F32, name="dbeta_part")
+        dbeta_over_beta = keep.tile([P, 8], F32, name="dbeta_over_beta")
+        sums_s = keep.tile([P, 2 * NCH, 8], F32, name="sums_s")
+        sums_v = keep.tile([P, 2 * NCH, 8], F32, name="sums_v")
 
-        A, V, GT, Q, M, WT, E2, SG = {}, {}, {}, {}, {}, {}, {}, {}
-        CHALF, ZSN, SHH, ER, TK, TKS, D16, GRP, TP, DG, MINI = {}, {}, {}, {}, {}, {}, {}, {}, {}, {}, {}
-        ZT = {}
+        A, V, G, Q, M, W, EM, SG = {}, {}, {}, {}, {}, {}, {}, {}
+        ER, C2, SH2, ZS2, ZROW, XROW = {}, {}, {}, {}, {}, {}
+        DXZ, FGRP, TP, HA, YS, T_CODES, T_SCALES, ACC, STAGE, TZ, SHCOL = {}, {}, {}, {}, {}, {}, {}, {}, {}, {}, {}
+        tail = []
 
         def cols(c):
             return slice(CH * c, CH * (c + 1))
 
-        def load_a(c, k):
-            A[(c, k)] = strm.tile([P, 2, 4, AW], F32, name="A", bufs=6)
+        def blocks(t):
+            return t[:].rearrange("p j (m o) -> p j m o", m=4)
+
+        def load_arg(c, k):
+            A[(c, k)] = ring.tile([P, 2, 4, BLK], F32, name="A", bufs=6)
             for jj in range(2):
                 nc.sync.dma_start(
                     out=A[(c, k)][:, jj, :, 0:P],
                     in_=arg_v[k // 2][:, 2 * (k % 2) + jj, cols(c)].rearrange("p (m o) -> p m o", m=4),
                 )
 
-        def fill_beta(c, k):
+        def put_beta(c, k):
             nc.gpsimd.tensor_copy(
                 out=A[(c, k)][:, :, :, P : P + 1],
                 in_=beta[:, 2 * k : 2 * k + 2].unsqueeze(2).unsqueeze(3).to_broadcast([P, 2, 4, 1]),
             )
 
-        def blocks(t):
-            return t[:].rearrange("p j (m o) -> p j m o", m=4)
-
-        def load_vg(c, k):
-            V[(c, k)] = strm.tile([P, 2, CH], F32, name="V", bufs=4)
+        def load_v_g(c, k):
+            V[(c, k)] = ring.tile([P, 2, CH], F32, name="V", bufs=4)
             nc.sync.dma_start(out=V[(c, k)][:], in_=v_v[k // 2][:, 2 * (k % 2) : 2 * (k % 2) + 2, cols(c)])
-            GT[(c, k)] = strm.tile([P, 2, CH], BF16, name="GT", bufs=4)
-            nc.sync.dma_start(out=GT[(c, k)][:], in_=go_v[k // 2][:, 2 * (k % 2) : 2 * (k % 2) + 2, cols(c)])
+            G[(c, k)] = ring.tile([P, 2, CH], BF16, name="G", bufs=4)
+            nc.sync.dma_start(out=G[(c, k)][:], in_=go_v[k // 2][:, 2 * (k % 2) : 2 * (k % 2) + 2, cols(c)])
 
-        def load_zt(c, m):
-            ZT[(c, m)] = strm.tile([P, D], BF16, name="ZT", bufs=4)
-            nc.sync.dma_start(out=ZT[(c, m)][:], in_=zn_v[c][:, m, :])
+        def load_z_rows(c):
+            for m in range(4):
+                ZROW[(c, m)] = ring.tile([P, D], BF16, name="ROW", bufs=4)
+                nc.sync.dma_start(out=ZROW[(c, m)][:], in_=z_rows[c][:, m, :])
 
-        def s_phase(c, k):
-            Q[(c, k)] = strm.tile([P, 2, CH], F32, name="Q", bufs=6)
-            WT[(c, k)] = strm.tile([P, 2, CH], F32, name="WT", bufs=2)
-            M[(c, k)] = strm.tile([P, 2, CH], F32, name="M", bufs=6)
+        def sqrt_phase(c, k):
+            Q[(c, k)] = ring.tile([P, 2, CH], F32, name="Q", bufs=6)
+            W[(c, k)] = ring.tile([P, 2, CH], F32, name="W", bufs=2)
+            M[(c, k)] = ring.tile([P, 2, CH], F32, name="M", bufs=6)
             nc.scalar.activation(out=blocks(Q[(c, k)]), in_=A[(c, k)][:, :, :, 0:P], func=ACT.Square)
             nc.scalar.activation(out=blocks(M[(c, k)]), in_=A[(c, k)][:, :, :, 0:P], func=ACT.Abs)
-            nc.scalar.activation(out=WT[(c, k)][:], in_=Q[(c, k)][:], func=ACT.Sqrt, bias=one_c[:])
+            nc.scalar.activation(out=W[(c, k)][:], in_=Q[(c, k)][:], func=ACT.Sqrt, bias=ones[:])
 
-        def u_op(c, k):
-            nc.vector.tensor_tensor(out=M[(c, k)][:], in0=M[(c, k)][:], in1=WT[(c, k)][:], op=ALU.add)
+        def add_abs_w(c, k):
+            nc.vector.tensor_tensor(out=M[(c, k)][:], in0=M[(c, k)][:], in1=W[(c, k)][:], op=ALU.add)
 
-        def zn_squares(c):
+        def zn_phase(c):
             for m in range(4):
                 nc.scalar.activation(
-                    out=ZT[(c, m)][:], in_=ZT[(c, m)][:], func=ACT.Square, accum_out=zs2[:, 4 * c + m : 4 * c + m + 1]
+                    out=ZROW[(c, m)][:], in_=ZROW[(c, m)][:], func=ACT.Square, accum_out=zsq[:, 4 * c + m : 4 * c + m + 1]
                 )
+            nc.scalar.activation(out=zn[:, 4 * c : 4 * c + 4], in_=zsq[:, 4 * c : 4 * c + 4], func=ACT.Sqrt)
 
-        def zn_sqrt(c):
-            nc.scalar.activation(out=zn[:, 4 * c : 4 * c + 4], in_=zs2[:, 4 * c : 4 * c + 4], func=ACT.Sqrt)
+        def rsqrt_phase(c, k):
+            nc.scalar.activation(out=Q[(c, k)][:], in_=Q[(c, k)][:], func=ACT.Abs_reciprocal_sqrt, bias=ones[:])
 
-        def r_phase(c, k):
-            nc.scalar.activation(out=Q[(c, k)][:], in_=Q[(c, k)][:], func=ACT.Abs_reciprocal_sqrt, bias=one_c[:])
-
-        def l_phase(c, k):
+        def ln_phase(c, k):
             nc.scalar.activation(out=M[(c, k)][:], in_=M[(c, k)][:], func=ACT.Ln)
 
-        def e_r(c):
-            ER[(c, 0)] = strm.tile([P, CH], F32, name="ER0", bufs=1)
-            ER[(c, 1)] = strm.tile([P, CH], F32, name="ER1", bufs=1)
-            nc.scalar.activation(out=ER[(c, 0)][:], in_=r_bc[:, cols(c)], func=ACT.Exp)
-            nc.scalar.activation(out=ER[(c, 1)][:], in_=r_bc[:, cols(c)], func=ACT.Exp, scale=-1.0)
+        def exp_r(c):
+            ER[(c, 0)] = ring.tile([P, CH], F32, name="ER0", bufs=1)
+            ER[(c, 1)] = ring.tile([P, CH], F32, name="ER1", bufs=1)
+            nc.scalar.activation(out=ER[(c, 0)][:], in_=r_rows[:, cols(c)], func=ACT.Exp)
+            nc.scalar.activation(out=ER[(c, 1)][:], in_=r_rows[:, cols(c)], func=ACT.Exp, scale=-1.0)
 
-        def e_phase(c, h):
-            for k in (2 * h, 2 * h + 1):
-                E2[(c, k)] = strm.tile([P, 2, CH], F32, name="E2", bufs=2)
-                nc.scalar.activation(out=E2[(c, k)][:], in_=V[(c, k)][:], func=ACT.Exp, scale=-1.0)
-            for k in (2 * h, 2 * h + 1):
+        def exp_phase(c, hf):
+            for k in (2 * hf, 2 * hf + 1):
+                EM[(c, k)] = ring.tile([P, 2, CH], F32, name="EM", bufs=2)
+                nc.scalar.activation(out=EM[(c, k)][:], in_=V[(c, k)][:], func=ACT.Exp, scale=-1.0)
+            for k in (2 * hf, 2 * hf + 1):
                 nc.scalar.activation(out=V[(c, k)][:], in_=V[(c, k)][:], func=ACT.Exp)
 
         def sign_phase(c, k):
-            SG[(c, k)] = strm.tile([P, 2, CH], BF16, name="SG", bufs=4)
+            SG[(c, k)] = ring.tile([P, 2, CH], BF16, name="SG", bufs=4)
             nc.scalar.activation(out=blocks(SG[(c, k)]), in_=A[(c, k)][:, :, :, 0:P], func=ACT.Sign)
 
-        def cz_pe(c):
-            bc = psum.tile([P, CH], F32, name="mx", bufs=3)
+        def zn_to_rows(c):
+            zrow = psum.tile([P, NB], F32, name="acc", bufs=AHEAD)
             for m in range(4):
                 nc.tensor.matmul(
-                    out=bc[:, P * m : P * (m + 1)],
-                    lhsT=zn[:, 4 * c + m : 4 * c + m + 1].to_broadcast([P, P]),
-                    rhs=ident[:],
-                    start=True,
-                    stop=True,
+                    out=zrow[:, P * m : P * (m + 1)], lhsT=zn[:, 4 * c + m : 4 * c + m + 1].to_broadcast([P, P]),
+                    rhs=ident[:], start=True, stop=True,
                 )
-            return bc
+            return zrow
 
-        def cz_dve1(c):
-            CHALF[c] = strm.tile([P, CH], F32, name="CHALF", bufs=1)
-            SHH[c] = strm.tile([P, CH], F32, name="SHH", bufs=1)
-            nc.vector.tensor_tensor(out=CHALF[c][:], in0=ER[(c, 0)][:], in1=ER[(c, 1)][:], op=ALU.add)
-            nc.vector.tensor_tensor(out=SHH[c][:], in0=ER[(c, 1)][:], in1=ER[(c, 0)][:], op=ALU.subtract)
+        def feature_rows(c, zrow):
+            C2[c] = ring.tile([P, CH], F32, name="C2", bufs=1)
+            SH2[c] = ring.tile([P, CH], F32, name="SH2", bufs=1)
+            ZS2[c] = ring.tile([P, CH], F32, name="ZS2", bufs=1)
+            nc.vector.tensor_tensor(out=C2[c][:], in0=ER[(c, 0)][:], in1=ER[(c, 1)][:], op=ALU.add)
+            nc.vector.tensor_tensor(out=SH2[c][:], in0=ER[(c, 1)][:], in1=ER[(c, 0)][:], op=ALU.subtract)
             nc.vector.reciprocal(out=rzn[:, 4 * c : 4 * c + 4], in_=zn[:, 4 * c : 4 * c + 4])
+            nc.vector.tensor_tensor(out=ZS2[c][:], in0=zrow[:], in1=SH2[c][:], op=ALU.mult)
 
-        def cz_pe2(c):
-            mn = psum.tile([P, CH], F32, name="mx", bufs=3)
+        def sinh_to_partitions(c):
+            SHCOL[c] = psum.tile([P, NB], F32, name="acc", bufs=AHEAD)
             for m in range(4):
                 nc.tensor.matmul(
-                    out=mn[:, m : m + 1], lhsT=SHH[c][:, P * m : P * (m + 1)], rhs=ident[:, 0:1], start=True, stop=True
+                    out=SHCOL[c][:, m : m + 1], lhsT=SH2[c][:, P * m : P * (m + 1)], rhs=ident[:, 0:1],
+                    start=True, stop=True,
                 )
-            return mn
 
-        def cz_dve2(c, bc):
-            ZSN[c] = strm.tile([P, CH], F32, name="ZSN", bufs=1)
-            nc.vector.tensor_tensor(out=ZSN[c][:], in0=bc[:], in1=SHH[c][:], op=ALU.mult)
-
-        def cz_dve3(c, mn):
-            nc.scalar.copy(out=shn[:, 4 * c : 4 * c + 4], in_=mn[:, 0:4])
+        def copy_sinh(c):
+            nc.scalar.copy(out=sh2n[:, 4 * c : 4 * c + 4], in_=SHCOL[c][:, 0:4])
 
         def chain_steps(c, k):
-            sg, vv, g2, q, mm, e2 = SG[(c, k)], V[(c, k)], GT[(c, k)], Q[(c, k)], M[(c, k)], E2[(c, k)]
-            h, jp = k // 2, k % 2
-            d16 = D16[(c, h)]
+            hf, jp = k // 2, k % 2
+            vv, q, mm = V[(c, k)], Q[(c, k)], M[(c, k)]
 
             def dbeta_step(jj):
-                junk = late.tile([P, CH], BF16, name="junk", bufs=2)
-                s = 4 * h + 2 * jp + jj
+                scrap = late.tile([P, CH], BF16, name="scrap", bufs=2)
                 nc.vector.scalar_tensor_tensor(
-                    out=junk[:], in0=q[:, jj, :], scalar=1.0, in1=ZSN[c][:], op0=ALU.mult, op1=ALU.mult,
-                    accum_out=dbp[:, s, c : c + 1],
+                    out=scrap[:], in0=q[:, jj, :], scalar=1.0, in1=ZS2[c][:], op0=ALU.mult, op1=ALU.mult,
+                    accum_out=dbeta_part[:, 4 * hf + 2 * jp + jj, c : c + 1],
                 )
 
             return [
-                lambda: nc.vector.tensor_tensor(out=vv[:], in0=vv[:], in1=e2[:], op=ALU.add),
+                lambda: nc.vector.tensor_tensor(out=vv[:], in0=vv[:], in1=EM[(c, k)][:], op=ALU.add),
                 lambda: nc.vector.scalar_tensor_tensor(
-                    out=vv[:], in0=vv[:], scalar=0.25, in1=g2[:], op0=ALU.mult, op1=ALU.mult
+                    out=vv[:], in0=vv[:], scalar=0.25, in1=G[(c, k)][:], op0=ALU.mult, op1=ALU.mult
                 ),
                 lambda: nc.vector.tensor_tensor(out=q[:], in0=vv[:], in1=q[:], op=ALU.mult),
                 lambda: nc.vector.tensor_tensor(
-                    out=d16[:, 2 * jp : 2 * jp + 2, :], in0=q[:],
-                    in1=CHALF[c][:].unsqueeze(1).to_broadcast([P, 2, CH]), op=ALU.mult,
+                    out=DXZ[(c, hf)][:, 2 * jp : 2 * jp + 2, :], in0=q[:],
+                    in1=C2[c][:].unsqueeze(1).to_broadcast([P, 2, CH]), op=ALU.mult,
                 ),
                 lambda: nc.vector.tensor_tensor(out=mm[:], in0=vv[:], in1=mm[:], op=ALU.mult),
                 lambda: dbeta_step(0),
-                lambda: nc.vector.tensor_tensor(out=mm[:], in0=mm[:], in1=sg[:], op=ALU.mult),
+                lambda: nc.vector.tensor_tensor(out=mm[:], in0=mm[:], in1=SG[(c, k)][:], op=ALU.mult),
                 lambda: dbeta_step(1),
             ]
 
-        def chain_pair(c, h, first, last, between):
+        def chain(c, hf, first, last, between):
             if first == 0:
-                D16[(c, h)] = late.tile([P, 4, CH], BF16, name="D16", bufs=2)
-            s0, s1 = chain_steps(c, 2 * h), chain_steps(c, 2 * h + 1)
+                DXZ[(c, hf)] = late.tile([P, 4, CH], BF16, name="DXZ", bufs=2)
+            even, odd = chain_steps(c, 2 * hf), chain_steps(c, 2 * hf + 1)
             for i in range(first, last):
-                s0[i]()
+                even[i]()
                 if between is not None:
-                    between(2 * (i - first))
-                s1[i]()
+                    between(2 * (i - 3))
+                odd[i]()
                 if between is not None:
-                    between(2 * (i - first) + 1)
+                    between(2 * (i - 3) + 1)
 
-        def pe_transposes(c, h):
-            for jp in range(2):
-                TP[(c, h, jp)] = psum.tile([P, 4, P], F32, name="tp", bufs=2)
-                for jj in range(2):
-                    words = D16[(c, h)][:, 2 * jp + jj, :].bitcast(F32)
-                    for u in range(2):
-                        nc.tensor.transpose(out=TP[(c, h, jp)][:, 2 * jj + u, :], in_=words[:, u::2], identity=ident[:])
-
-        def evac(c, h):
-            GRP[(c, h)] = late.tile([P, CH, 4], BF16, name="GRP", bufs=1, align_bytes=64)
-            gw = GRP[(c, h)][:].rearrange("p t e -> p (t e)").bitcast(F32).rearrange("p (j r u) -> p j r u", j=4, u=2)
-            for jp in range(2):
-                nc.scalar.copy(
-                    out=gw[:, 2 * jp : 2 * jp + 2, :, :],
-                    in_=TP[(c, h, jp)][:].rearrange("p (jj u) r -> p jj r u", u=2),
-                )
-
-        def pe_diag(c, h):
+        def h_arg_products(c, hf):
             for m in range(4):
-                blk = slice(P * m, P * (m + 1))
                 if m % 2 == 0:
-                    dgt = psum.tile([P, 512], F32, name="dg", bufs=2)
-                    DG[(c, h, m // 2)] = dgt[:, 0 : 2 * AW].rearrange("p (m w) -> p m w", m=2)
+                    bank = psum.tile([P, NB], F32, name="ha", bufs=2)
+                    HA[(c, hf, m // 2)] = bank[:, 0 : 2 * BLK].rearrange("p (m w) -> p m w", m=2)
                 for j in range(4):
-                    k = 2 * h + j // 2
+                    k = 2 * hf + j // 2
                     nc.tensor.matmul(
-                        out=DG[(c, h, m // 2)][:, m % 2, 0 : P + 1], lhsT=Q[(c, k)][:, j % 2, blk],
+                        out=HA[(c, hf, m // 2)][:, m % 2, 0 : P + 1], lhsT=Q[(c, k)][:, j % 2, P * m : P * (m + 1)],
                         rhs=A[(c, k)][:, j % 2, m, 0 : P + 1], start=(j == 0), stop=(j == 3),
                     )
 
-        def pe_minis(c, h):
-            MINI[(c, h)] = psum.tile([P, 16], F32, name="mini", bufs=1)
+        def y_sums(c, hf):
+            YS[(c, hf)] = psum.tile([P, 16], F32, name="ys", bufs=1)
             for m in range(4):
-                blk = slice(P * m, P * (m + 1))
                 for j in range(4):
-                    k = 2 * h + j // 2
+                    k = 2 * hf + j // 2
                     nc.tensor.matmul(
-                        out=MINI[(c, h)][:, m : m + 1], lhsT=M[(c, k)][:, j % 2, blk], rhs=one_c[:],
+                        out=YS[(c, hf)][:, m : m + 1], lhsT=M[(c, k)][:, j % 2, P * m : P * (m + 1)], rhs=ones[:],
                         start=(j == 0), stop=(j == 3),
                     )
 
-        def post_tk(c, h):
-            if h == 0:
-                TK[c] = strm.tile([P, 2, CH], U32, name="TK", bufs=2, align_bytes=64)
-                TKS[c] = strm.tile([P, 2, CH], U8, name="TKS", bufs=2, align_bytes=64)
-            di = late.tile([P, CH, 4], BF16, name="DI", bufs=1, align_bytes=64)
-            nc.vector.tensor_copy(out=di[:], in_=D16[(c, h)][:].rearrange("p j o -> p o j"))
-            return di
+        def transposes(c, hf):
+            for jp in range(2):
+                TP[(c, hf, jp)] = psum.tile([P, 4, P], F32, name="tp", bufs=2)
+                for jj in range(2):
+                    words = DXZ[(c, hf)][:, 2 * jp + jj, :].bitcast(F32)
+                    for u in range(2):
+                        nc.tensor.transpose(out=TP[(c, hf, jp)][:, 2 * jj + u, :], in_=words[:, u::2], identity=ident[:])
 
-        def post_tk_q(c, h, di):
+        def copy_transposed(c, hf):
+            FGRP[(c, hf)] = late.tile([P, CH, 4], BF16, name="FGRP", bufs=1, align_bytes=64)
+            words = FGRP[(c, hf)][:].rearrange("p t e -> p (t e)").bitcast(F32).rearrange("p (j r u) -> p j r u", j=4, u=2)
+            for jp in range(2):
+                nc.scalar.copy(
+                    out=words[:, 2 * jp : 2 * jp + 2, :, :], in_=TP[(c, hf, jp)][:].rearrange("p (jj u) r -> p jj r u", u=2)
+                )
+
+        def group_tokens(c, hf):
+            if hf == 0:
+                T_CODES[c] = ring.tile([P, 2, CH], U32, name="T_CODES", bufs=2, align_bytes=64)
+                T_SCALES[c] = ring.tile([P, 2, CH], U8, name="T_SCALES", bufs=2, align_bytes=64)
+            tgrp = late.tile([P, CH, 4], BF16, name="TGRP", bufs=1, align_bytes=64)
+            nc.vector.tensor_copy(out=tgrp[:], in_=DXZ[(c, hf)][:].rearrange("p j o -> p o j"))
+            return tgrp
+
+        def quantize_tokens(c, hf, tgrp):
             nc.vector.quantize_mx(
-                out=TK[c][:, h, :].bitcast(E5), scales=TKS[c][:, h, :], in_=di[:].rearrange("p o j -> p (o j)")
+                out=T_CODES[c][:, hf, :].bitcast(E5M2), scales=T_SCALES[c][:, hf, :],
+                in_=tgrp[:].rearrange("p o j -> p (o j)"),
             )
 
-        def post_ft_q(c, h):
+        def quantize_features(c, hf):
             nc.vector.quantize_mx(
-                out=ft_codes[:, c, CH * h : CH * (h + 1)].bitcast(E5), scales=ft_scales[:, c, CH * h : CH * (h + 1)],
-                in_=GRP[(c, h)][:].rearrange("p t e -> p (t e)"),
+                out=f_codes[:, c, CH * hf : CH * (hf + 1)].bitcast(E5M2), scales=f_scales[:, c, CH * hf : CH * (hf + 1)],
+                in_=FGRP[(c, hf)][:].rearrange("p t e -> p (t e)"),
             )
 
-        def post_sums(c, h):
+        def read_h_arg(c, hf):
             for m in range(4):
-                jk = late.tile([P, P], F32, name="jk", bufs=4)
+                scrap = late.tile([P, P], F32, name="scrap_d", bufs=4)
                 nc.vector.scalar_tensor_tensor(
-                    out=jk[:], in0=DG[(c, h, m // 2)][:, m % 2, 0:P], scalar=1.0, in1=ident[:], op0=ALU.mult,
-                    op1=ALU.mult, accum_out=sums_d[:, 2 * c + h, m : m + 1],
+                    out=scrap[:], in0=HA[(c, hf, m // 2)][:, m % 2, 0:P], scalar=1.0, in1=ident[:], op0=ALU.mult,
+                    op1=ALU.mult, accum_out=sums_v[:, 2 * c + hf, m : m + 1],
                 )
             for mp in range(2):
                 nc.scalar.copy(
-                    out=sums_a[:, 2 * c + h, 4 + 2 * mp : 6 + 2 * mp],
-                    in_=DG[(c, h, mp)][:, :, P : P + 1].rearrange("p m one -> p (m one)"),
+                    out=sums_s[:, 2 * c + hf, 4 + 2 * mp : 6 + 2 * mp],
+                    in_=HA[(c, hf, mp)][:, :, P : P + 1].rearrange("p m one -> p (m one)"),
                 )
 
-        def post_mini(c, h):
-            nc.scalar.copy(out=sums_a[:, 2 * c + h, 0:4], in_=MINI[(c, h)][:, 0:4])
+        def read_y_sums(c, hf):
+            nc.scalar.copy(out=sums_s[:, 2 * c + hf, 0:4], in_=YS[(c, hf)][:, 0:4])
 
-        def fin_small(c):
-            s8 = keep.tile([P, 8], F32, name="s8", bufs=2)
-            t2 = keep.tile([P, 4], F32, name="t2", bufs=2)
+        def t_over_zn(c):
+            both = keep.tile([P, 8], F32, name="both", bufs=2)
+            harg = keep.tile([P, 4], F32, name="harg", bufs=2)
             ta = keep.tile([P, 4], F32, name="ta", bufs=2)
             tb = keep.tile([P, 4], F32, name="tb", bufs=2)
-            tz = keep.tile([P, 4], F32, name="tz", bufs=2)
-            nc.gpsimd.tensor_tensor(out=s8[:], in0=sums_a[:, 2 * c, :], in1=sums_a[:, 2 * c + 1, :], op=ALU.add)
-            nc.gpsimd.tensor_tensor(out=t2[:], in0=sums_d[:, 2 * c, 0:4], in1=sums_d[:, 2 * c + 1, 0:4], op=ALU.add)
-            nc.gpsimd.tensor_tensor(out=ta[:], in0=s8[:, 0:4], in1=t2[:], op=ALU.subtract)
-            nc.gpsimd.tensor_tensor(out=tb[:], in0=s8[:, 4:8], in1=shn[:, 4 * c : 4 * c + 4], op=ALU.mult)
+            TZ[c] = keep.tile([P, 4], F32, name="tz", bufs=2)
+            nc.gpsimd.tensor_tensor(out=both[:], in0=sums_s[:, 2 * c, :], in1=sums_s[:, 2 * c + 1, :], op=ALU.add)
+            nc.gpsimd.tensor_tensor(out=harg[:], in0=sums_v[:, 2 * c, 0:4], in1=sums_v[:, 2 * c + 1, 0:4], op=ALU.add)
+            nc.gpsimd.tensor_tensor(out=ta[:], in0=both[:, 0:4], in1=harg[:], op=ALU.subtract)
+            nc.gpsimd.tensor_tensor(out=tb[:], in0=both[:, 4:8], in1=sh2n[:, 4 * c : 4 * c + 4], op=ALU.mult)
             nc.gpsimd.tensor_tensor(out=ta[:], in0=ta[:], in1=ta[:], op=ALU.add)
             nc.gpsimd.tensor_tensor(out=ta[:], in0=ta[:], in1=tb[:], op=ALU.add)
-            nc.gpsimd.tensor_tensor(out=tz[:], in0=ta[:], in1=rzn[:, 4 * c : 4 * c + 4], op=ALU.mult)
-            return tz
+            nc.gpsimd.tensor_tensor(out=TZ[c][:], in0=ta[:], in1=rzn[:, 4 * c : 4 * c + 4], op=ALU.mult)
 
-        PS, OST, XE = {}, {}, {}
-        TAIL = []
+        def accumulator():
+            if len(tail) == 0:
+                return psum.tile([P, NB], F32, name="acc", bufs=AHEAD)
+            turn = (len(tail) - 1) % TAIL_BANKS
+            tail.append(0)
+            if turn < AHEAD:
+                return psum.tile([P, NB], F32, name="acc", bufs=AHEAD)
+            if turn < AHEAD + 2:
+                bank = psum.tile([P, 4, P], F32, name="tp", bufs=2)
+                return bank[:].rearrange("p a b -> p (a b)")
+            return psum.tile([P, NB], F32, name="ha", bufs=2)
 
-        def acc_tile():
-            if len(TAIL) == 0:
-                return psum.tile([P, 512], F32, name="mx", bufs=3)
-            which = (len(TAIL) - 1) % 7
-            TAIL.append(0)
-            if which < 3:
-                return psum.tile([P, 512], F32, name="mx", bufs=3)
-            if which < 5:
-                tpt = psum.tile([P, 4, P], F32, name="tp", bufs=2)
-                return tpt[:].rearrange("p a b -> p (a b)")
-            return psum.tile([P, 512], F32, name="dg", bufs=2)
+        def staging():
+            if len(tail) == 0:
+                return late.tile([P, D], F32, name="stage", bufs=2)
+            row = ring.tile([P, 2, CH], F32, name="Q", bufs=6)
+            return row[:].rearrange("p a b -> p (a b)")
 
-
-        def ost_tile():
-            if len(TAIL) == 0:
-                return late.tile([P, D], F32, name="ost", bufs=2)
-            qt = strm.tile([P, 2, CH], F32, name="Q", bufs=6)
-            return qt[:].rearrange("p a b -> p (a b)")
-
-        def out1_pe(c, i):
+        def out1_product(c, i):
             m, dh = i // 2, i % 2
-            PS[("o1", c, i)] = acc_tile()
+            ACC[("out1", c, i)] = accumulator()
             for g in range(2):
                 nc.tensor.matmul_mx(
-                    out=PS[("o1", c, i)][:],
-                    lhsT=TK[c][:, g, P * m : P * (m + 1)].bitcast(E5),
-                    lhsT_scale=TKS[c][:, g, P * m : P * (m + 1)],
-                    rhs=x_codes[:, g, 512 * dh : 512 * (dh + 1)].bitcast(E4),
-                    rhs_scale=x_scales[:, g, 512 * dh : 512 * (dh + 1)],
+                    out=ACC[("out1", c, i)][:],
+                    lhsT=T_CODES[c][:, g, P * m : P * (m + 1)].bitcast(E5M2),
+                    lhsT_scale=T_SCALES[c][:, g, P * m : P * (m + 1)],
+                    rhs=x_codes[:, g, NB * dh : NB * (dh + 1)].bitcast(E4M3),
+                    rhs_scale=x_scales[:, g, NB * dh : NB * (dh + 1)],
                     start=(g == 0), stop=(g == 1),
                 )
 
-        def out1_dve(c, i):
+        def out1_epilogue(c, i):
             m, dh = i // 2, i % 2
             if dh == 0:
-                OST[("o1", c, m)] = ost_tile()
-            ost = OST[("o1", c, m)]
+                STAGE[("out1", c, m)] = staging()
+            row = STAGE[("out1", c, m)]
             nc.vector.scalar_tensor_tensor(
-                out=ost[:, 512 * dh : 512 * (dh + 1)], in0=ZT[(c, m)][:, 512 * dh : 512 * (dh + 1)],
-                scalar=TZ[c][:, m : m + 1], in1=PS[("o1", c, i)][:], op0=ALU.mult, op1=ALU.add,
+                out=row[:, NB * dh : NB * (dh + 1)], in0=ZROW[(c, m)][:, NB * dh : NB * (dh + 1)],
+                scalar=TZ[c][:, m : m + 1], in1=ACC[("out1", c, i)][:], op0=ALU.mult, op1=ALU.add,
             )
             if dh == 1:
-                nc.sync.dma_start(out=o1_v[c][:, m, :], in_=ost[:])
+                nc.sync.dma_start(out=out1_v[c][:, m, :], in_=row[:])
 
-        def load_xe(g, j):
-            XE[(g, j)] = late.tile([P, D], BF16, name="xe", bufs=2)
-            nc.sync.dma_start(out=XE[(g, j)][:], in_=x_v[g][:, j, :])
+        def load_x_row(g, j):
+            XROW[(g, j)] = late.tile([P, D], BF16, name="XROW", bufs=2)
+            nc.sync.dma_start(out=XROW[(g, j)][:], in_=x_v[g][:, j, :])
 
-        def out0_scale(g):
-            dbs = keep.tile([P, 4], F32, name="dbs", bufs=2)
-            nc.vector.tensor_reduce(out=dbs[:], in_=dbp[:, 4 * g : 4 * g + 4, :], axis=AX.X, op=ALU.add)
-            nc.vector.tensor_tensor(out=sb[:, 4 * g : 4 * g + 4], in0=dbs[:], in1=rbeta[:, 4 * g : 4 * g + 4], op=ALU.mult)
+        def out0_factor(g):
+            total = keep.tile([P, 4], F32, name="total", bufs=2)
+            nc.vector.tensor_reduce(out=total[:], in_=dbeta_part[:, 4 * g : 4 * g + 4, :], axis=AX.X, op=ALU.add)
+            nc.vector.tensor_tensor(
+                out=dbeta_over_beta[:, 4 * g : 4 * g + 4], in0=total[:], in1=rbeta[:, 4 * g : 4 * g + 4], op=ALU.mult
+            )
 
-        def out0_pe(g, i):
+        def out0_product(g, i):
             s, dh = 4 * g + i // 2, i % 2
-            PS[("o0", g, i)] = acc_tile()
-            for c in range(NG):
+            ACC[("out0", g, i)] = accumulator()
+            for c in range(NCH):
                 nc.tensor.matmul_mx(
-                    out=PS[("o0", g, i)][:],
-                    lhsT=ft_codes[:, c, P * s : P * (s + 1)].bitcast(E5),
-                    lhsT_scale=ft_scales[:, c, P * s : P * (s + 1)],
-                    rhs=z_codes[:, c, 512 * dh : 512 * (dh + 1)].bitcast(E4),
-                    rhs_scale=z_scales[:, c, 512 * dh : 512 * (dh + 1)],
-                    start=(c == 0), stop=(c == NG - 1),
+                    out=ACC[("out0", g, i)][:],
+                    lhsT=f_codes[:, c, P * s : P * (s + 1)].bitcast(E5M2),
+                    lhsT_scale=f_scales[:, c, P * s : P * (s + 1)],
+                    rhs=z_codes[:, c, NB * dh : NB * (dh + 1)].bitcast(E4M3),
+                    rhs_scale=z_scales[:, c, NB * dh : NB * (dh + 1)],
+                    start=(c == 0), stop=(c == NCH - 1),
                 )
 
-        def out0_dve(g, i):
+        def out0_epilogue(g, i):
             j, dh = i // 2, i % 2
             if dh == 0:
-                OST[("o0", g, j)] = ost_tile()
-            ost = OST[("o0", g, j)]
+                STAGE[("out0", g, j)] = staging()
+            row = STAGE[("out0", g, j)]
             nc.vector.scalar_tensor_tensor(
-                out=ost[:, 512 * dh : 512 * (dh + 1)], in0=XE[(g, j)][:, 512 * dh : 512 * (dh + 1)],
-                scalar=sb[:, 4 * g + j : 4 * g + j + 1], in1=PS[("o0", g, i)][:], op0=ALU.mult, op1=ALU.add,
+                out=row[:, NB * dh : NB * (dh + 1)], in0=XROW[(g, j)][:, NB * dh : NB * (dh + 1)],
+                scalar=dbeta_over_beta[:, 4 * g + j : 4 * g + j + 1], in1=ACC[("out0", g, i)][:],
+                op0=ALU.mult, op1=ALU.add,
             )
             if dh == 1:
-                nc.sync.dma_start(out=o0_v[g][:, j, :], in_=ost[:])
+                nc.sync.dma_start(out=out0_v[g][:, j, :], in_=row[:])
                 if j + 2 < 4:
-                    load_xe(g, j + 2)
+                    load_x_row(g, j + 2)
 
         with tc.tile_pool(name="prep", bufs=2) as prep:
             RAW = {}
@@ -400,225 +392,217 @@ def tile_pvfc_v_kernel(tc, x, z, r, bias, arg, v, grad_out, out_0, out_1):
                 RAW[key] = prep.tile([P, 4, D], BF16, name="raw", bufs=2)
                 nc.sync.dma_start(out=RAW[key][:], in_=src)
 
-            def prep_copy(key):
-                grps = []
+            def group_rows(key):
+                halves = []
                 for dh in range(2):
-                    grp = prep.tile([P, 512, 4], BF16, name="pgrp", bufs=2, align_bytes=64)
+                    grp = prep.tile([P, NB, 4], BF16, name="grp", bufs=2, align_bytes=64)
                     nc.vector.tensor_copy(
-                        out=grp[:], in_=RAW[key][:, :, 512 * dh : 512 * (dh + 1)].rearrange("p j d -> p d j")
+                        out=grp[:], in_=RAW[key][:, :, NB * dh : NB * (dh + 1)].rearrange("p j d -> p d j")
                     )
-                    grps.append(grp)
-                return grps
+                    halves.append(grp)
+                return halves
 
-            def prep_quant(grps, codes, scales):
+            def quantize_rows(halves, codes, scales):
                 for dh in range(2):
                     nc.vector.quantize_mx(
-                        out=codes[:, 512 * dh : 512 * (dh + 1)].bitcast(E4), scales=scales[:, 512 * dh : 512 * (dh + 1)],
-                        in_=grps[dh][:].rearrange("p d j -> p (d j)"),
+                        out=codes[:, NB * dh : NB * (dh + 1)].bitcast(E4M3), scales=scales[:, NB * dh : NB * (dh + 1)],
+                        in_=halves[dh][:].rearrange("p d j -> p (d j)"),
                     )
 
-            def x_squares(g):
-                for j in range(4):
-                    xj = prep.tile([P, D], BF16, name="xj", bufs=2)
-                    nc.vector.scalar_tensor_tensor(
-                        out=xj[:], in0=RAW[("x", g)][:, j, :], scalar=1.0, in1=RAW[("x", g)][:, j, :],
-                        op0=ALU.mult, op1=ALU.mult, accum_out=xs[:, 4 * g + j : 4 * g + j + 1],
-                    )
-
-            load_a(0, 0)
-            load_a(0, 1)
+            load_arg(0, 0)
+            load_arg(0, 1)
             load_raw(("x", 0), x_v[0])
-            load_a(0, 2)
-            load_a(0, 3)
+            load_arg(0, 2)
+            load_arg(0, 3)
             load_raw(("x", 1), x_v[1])
-            for m in range(4):
-                load_zt(0, m)
-            nc.sync.dma_start(out=r_bc[:], in_=r.rearrange("o one -> (o one)").partition_broadcast(P))
+            load_z_rows(0)
+            nc.sync.dma_start(out=r_rows[:], in_=r.rearrange("o one -> (o one)").partition_broadcast(P))
             for k in range(4):
-                load_vg(0, k)
-            s_phase(0, 0)
-            s_phase(0, 1)
-            g0 = prep_copy(("x", 0))
-            u_op(0, 0)
-            u_op(0, 1)
-            s_phase(0, 2)
-            s_phase(0, 3)
-            x_squares(0)
-            zn_squares(0)
-            zn_sqrt(0)
-            nc.scalar.activation(out=beta[:, 0:4], in_=xs[:, 0:4], func=ACT.Sqrt, bias=one_c[:])
-            fill_beta(0, 0)
-            fill_beta(0, 1)
-            prep_quant(g0, x_codes[:, 0, :], x_scales[:, 0, :])
-            load_raw(("z", 0), zq_v[0])
-            u_op(0, 2)
-            u_op(0, 3)
+                load_v_g(0, k)
+            sqrt_phase(0, 0)
+            sqrt_phase(0, 1)
+            x0 = group_rows(("x", 0))
+            add_abs_w(0, 0)
+            add_abs_w(0, 1)
+            sqrt_phase(0, 2)
+            sqrt_phase(0, 3)
+            for j in range(4):
+                scrap = prep.tile([P, D], BF16, name="scrap_x", bufs=2)
+                nc.vector.scalar_tensor_tensor(
+                    out=scrap[:], in0=RAW[("x", 0)][:, j, :], scalar=1.0, in1=RAW[("x", 0)][:, j, :],
+                    op0=ALU.mult, op1=ALU.mult, accum_out=xsq_v[:, j : j + 1],
+                )
+            zn_phase(0)
+            nc.scalar.activation(out=beta[:, 0:4], in_=xsq_v[:], func=ACT.Sqrt, bias=ones[:])
+            put_beta(0, 0)
+            put_beta(0, 1)
+            quantize_rows(x0, x_codes[:, 0, :], x_scales[:, 0, :])
+            load_raw(("z", 0), z_k[0])
+            add_abs_w(0, 2)
+            add_abs_w(0, 3)
             for k in range(4):
-                r_phase(0, k)
+                rsqrt_phase(0, k)
             for k in range(4):
-                l_phase(0, k)
-            e_r(0)
-            e_phase(0, 0)
+                ln_phase(0, k)
+            exp_r(0)
+            exp_phase(0, 0)
             sign_phase(0, 0)
             sign_phase(0, 1)
             for j in range(4):
-                xt = strm.tile([P, D], BF16, name="ZT", bufs=4)
-                nc.sync.dma_start(out=xt[:], in_=x_v[1][:, j, :])
-                nc.scalar.activation(out=xt[:], in_=xt[:], func=ACT.Square, accum_out=xs2[:, j : j + 1])
-            g1 = prep_copy(("x", 1))
-            prep_quant(g1, x_codes[:, 1, :], x_scales[:, 1, :])
-            load_raw(("z", 1), zq_v[1])
-            for c in range(NG):
-                g0 = prep_copy(("z", c))
-                if c + 2 < NG:
-                    load_raw(("z", c + 2), zq_v[c + 2])
-                prep_quant(g0, z_codes[:, c, :], z_scales[:, c, :])
-            load_a(1, 0)
-            load_a(1, 1)
+                xrow = ring.tile([P, D], BF16, name="ROW", bufs=4)
+                nc.sync.dma_start(out=xrow[:], in_=x_v[1][:, j, :])
+                nc.scalar.activation(out=xrow[:], in_=xrow[:], func=ACT.Square, accum_out=xsq_s[:, j : j + 1])
+            x1 = group_rows(("x", 1))
+            quantize_rows(x1, x_codes[:, 1, :], x_scales[:, 1, :])
+            load_raw(("z", 1), z_k[1])
+            for c in range(NCH):
+                zc = group_rows(("z", c))
+                if c + 2 < NCH:
+                    load_raw(("z", c + 2), z_k[c + 2])
+                quantize_rows(zc, z_codes[:, c, :], z_scales[:, c, :])
+            load_arg(1, 0)
+            load_arg(1, 1)
 
         late = ctx.enter_context(tc.tile_pool(name="late", bufs=2))
-        bc0 = cz_pe(0)
-        cz_dve1(0)
-        mn0 = cz_pe2(0)
-        cz_dve2(0, bc0)
-        cz_dve3(0, mn0)
+        feature_rows(0, zn_to_rows(0))
+        sinh_to_partitions(0)
+        copy_sinh(0)
 
-        TZ, MN = {}, {}
-        LAST = 2 * NG - 1
-        AHEAD = 3
-        for hh in range(2 * NG):
-            c, h = hh // 2, hh % 2
+        last = 2 * NCH - 1
+        for n in range(2 * NCH):
+            c, hf = n // 2, n % 2
             nx = c + 1
-            more = nx < NG
-            pc, ph = (hh - 1) // 2, (hh - 1) % 2
-            if h == 0 and c >= 1:
-                wpe, wdve = (lambda i: out1_pe(c - 1, i)), (lambda i: out1_dve(c - 1, i))
-                weave = 8
-            elif hh == LAST:
-                wpe, wdve = (lambda i: out0_pe(0, i)), (lambda i: out0_dve(0, i))
-                weave = 8
+            more = nx < NCH
+            pc, ph = (n - 1) // 2, (n - 1) % 2
+
+            if hf == 0 and c >= 1:
+                product, epilogue = (lambda i: out1_product(c - 1, i)), (lambda i: out1_epilogue(c - 1, i))
+                groups = 8
+            elif n == last:
+                product, epilogue = (lambda i: out0_product(0, i)), (lambda i: out0_epilogue(0, i))
+                groups = 8
             else:
-                wpe, wdve = None, None
-                weave = 0
+                product, epilogue = None, None
+                groups = 0
 
-            def woven(t):
-                i = t if t < AHEAD else t - 2
-                if i < weave and t != AHEAD and t != AHEAD + 1:
-                    wdve(i)
-                    if i + AHEAD < weave:
-                        wpe(i + AHEAD)
+            def woven(place):
+                i = place if place < AHEAD else place - 2
+                if i < groups and place != AHEAD and place != AHEAD + 1:
+                    epilogue(i)
+                    if i + AHEAD < groups:
+                        product(i + AHEAD)
 
-            if hh >= 1:
-                post_sums(pc, ph)
-                if h == 0:
-                    cz_dve3(c, MN[c])
-            for i in range(min(AHEAD, weave)):
-                wpe(i)
-            chain_pair(c, h, 0, 1, None)
-            if hh >= 1:
-                post_mini(pc, ph)
-                if h == 0:
-                    TZ[pc] = fin_small(pc)
-            chain_pair(c, h, 1, 3, None)
-            if h == 0:
-                e_phase(c, 1)
+            if n >= 1:
+                read_h_arg(pc, ph)
+                if hf == 0:
+                    copy_sinh(c)
+            for i in range(min(AHEAD, groups)):
+                product(i)
+            chain(c, hf, 0, 1, None)
+            if n >= 1:
+                read_y_sums(pc, ph)
+                if hf == 0:
+                    t_over_zn(pc)
+            chain(c, hf, 1, 3, None)
+            if hf == 0:
+                exp_phase(c, 1)
                 sign_phase(c, 2)
                 sign_phase(c, 3)
                 if more:
-                    e_r(nx)
-            if hh == 0:
-                nc.scalar.activation(out=beta[:, 4:8], in_=xs2[:], func=ACT.Sqrt, bias=one_c[:])
-                fill_beta(0, 2)
-                fill_beta(0, 3)
-                fill_beta(1, 0)
-                fill_beta(1, 1)
-            pe_diag(c, h)
-            if more and h == 0:
-                s_phase(nx, 0)
-                s_phase(nx, 1)
-                load_a(nx, 2)
-                load_a(nx, 3)
-                fill_beta(nx, 2)
-                fill_beta(nx, 3)
-            if more and h == 1:
-                u_op(nx, 2)
-                u_op(nx, 3)
-                bcn = cz_pe(nx)
+                    exp_r(nx)
+            if n == 0:
+                nc.scalar.activation(out=beta[:, 4:8], in_=xsq_s[:], func=ACT.Sqrt, bias=ones[:])
+                put_beta(0, 2)
+                put_beta(0, 3)
+                put_beta(1, 0)
+                put_beta(1, 1)
+            h_arg_products(c, hf)
+            if more and hf == 0:
+                sqrt_phase(nx, 0)
+                sqrt_phase(nx, 1)
+                load_arg(nx, 2)
+                load_arg(nx, 3)
+                put_beta(nx, 2)
+                put_beta(nx, 3)
+            if more and hf == 1:
+                add_abs_w(nx, 2)
+                add_abs_w(nx, 3)
+                zrow = zn_to_rows(nx)
                 for k in range(4):
-                    r_phase(nx, k)
-                if nx + 1 < NG:
-                    load_a(nx + 1, 0)
-                    load_a(nx + 1, 1)
-                    fill_beta(nx + 1, 0)
-                    fill_beta(nx + 1, 1)
-            if hh == LAST:
-                chain_pair(c, h, 3, 4, woven)
-                pe_transposes(c, h)
-                evac(c, h)
-                chain_pair(c, h, 4, 8, lambda t: woven(t + 2))
-                pe_minis(c, h)
+                    rsqrt_phase(nx, k)
+                if nx + 1 < NCH:
+                    load_arg(nx + 1, 0)
+                    load_arg(nx + 1, 1)
+                    put_beta(nx + 1, 0)
+                    put_beta(nx + 1, 1)
+            if n == last:
+                chain(c, hf, 3, 4, woven)
+                transposes(c, hf)
+                copy_transposed(c, hf)
+                chain(c, hf, 4, 8, woven)
+                y_sums(c, hf)
             else:
-                chain_pair(c, h, 3, 8, woven)
-                pe_minis(c, h)
-                if hh >= 1:
-                    evac(pc, ph)
-                pe_transposes(c, h)
-            if hh == 0:
+                chain(c, hf, 3, 8, woven)
+                y_sums(c, hf)
+                if n >= 1:
+                    copy_transposed(pc, ph)
+                transposes(c, hf)
+            if n == 0:
                 nc.vector.reciprocal(out=rbeta[:], in_=beta[:])
-            if more and h == 0:
-                load_vg(nx, 0)
-                load_vg(nx, 1)
-                for m in range(4):
-                    load_zt(nx, m)
-                u_op(nx, 0)
-                u_op(nx, 1)
-                s_phase(nx, 2)
-                s_phase(nx, 3)
-                zn_squares(nx)
-                zn_sqrt(nx)
-            if more and h == 1:
+            if more and hf == 0:
+                load_v_g(nx, 0)
+                load_v_g(nx, 1)
+                load_z_rows(nx)
+                add_abs_w(nx, 0)
+                add_abs_w(nx, 1)
+                sqrt_phase(nx, 2)
+                sqrt_phase(nx, 3)
+                zn_phase(nx)
+            if more and hf == 1:
                 for k in range(4):
-                    l_phase(nx, k)
-                load_vg(nx, 2)
-                load_vg(nx, 3)
-                e_phase(nx, 0)
+                    ln_phase(nx, k)
+                load_v_g(nx, 2)
+                load_v_g(nx, 3)
+                exp_phase(nx, 0)
                 sign_phase(nx, 0)
                 sign_phase(nx, 1)
-            di = post_tk(c, h)
-            if hh >= 1 and hh != LAST:
-                post_ft_q(pc, ph)
-            post_tk_q(c, h, di)
-            if h == 1:
+            tgrp = group_tokens(c, hf)
+            if n >= 1 and n != last:
+                quantize_features(pc, ph)
+            quantize_tokens(c, hf, tgrp)
+            if hf == 1:
                 if more:
-                    cz_dve1(nx)
-                    cz_dve2(nx, bcn)
-                    MN[nx] = cz_pe2(nx)
-                for m in range(4):
-                    load_zt(c, m)
-            if hh == LAST - 1:
-                load_xe(0, 0)
-                load_xe(0, 1)
-                evac(c, h)
-                post_ft_q(c, h)
-                out0_scale(0)
-        load_xe(1, 0)
-        load_xe(1, 1)
-        post_ft_q(NG - 1, 1)
-        out0_scale(1)
-        post_sums(NG - 1, 1)
-        post_mini(NG - 1, 1)
-        TZ[NG - 1] = fin_small(NG - 1)
-        TAIL.append(0)
-        DEEP = 7
-        for i in range(DEEP):
-            out0_pe(1, i)
+                    feature_rows(nx, zrow)
+                    sinh_to_partitions(nx)
+                load_z_rows(c)
+            if n == last - 1:
+                load_x_row(0, 0)
+                load_x_row(0, 1)
+                copy_transposed(c, hf)
+                quantize_features(c, hf)
+                out0_factor(0)
+
+        load_x_row(1, 0)
+        load_x_row(1, 1)
+        quantize_features(NCH - 1, 1)
+        out0_factor(1)
+        read_h_arg(NCH - 1, 1)
+        read_y_sums(NCH - 1, 1)
+        t_over_zn(NCH - 1)
+        tail.append(0)
+
+        def tail_product(i):
+            if i < 8:
+                out0_product(1, i)
+            else:
+                out1_product(NCH - 1, i - 8)
+
+        for i in range(TAIL_BANKS):
+            tail_product(i)
         for i in range(16):
             if i < 8:
-                out0_dve(1, i)
+                out0_epilogue(1, i)
             else:
-                out1_dve(NG - 1, i - 8)
-            n = i + DEEP
-            if n < 8:
-                out0_pe(1, n)
-            elif n < 16:
-                out1_pe(NG - 1, n - 8)
+                out1_epilogue(NCH - 1, i - 8)
+            if i + TAIL_BANKS < 16:
+                tail_product(i + TAIL_BANKS)

@@ -258,7 +258,9 @@ def tile_pvfc_v_kernel(tc, x, z, r, bias, arg, v, grad_out, out_0, out_1):
                 T_CODES[c] = ring.tile([P, 2, CH], U32, name="T_CODES", bufs=2, align_bytes=64)
                 T_SCALES[c] = ring.tile([P, 2, CH], U8, name="T_SCALES", bufs=2, align_bytes=64)
             tgrp = late.tile([P, CH, 4], BF16, name="TGRP", bufs=1, align_bytes=64)
-            nc.vector.tensor_copy(out=tgrp[:], in_=DXZ[(c, hf)][:].rearrange("p j o -> p o j"))
+            nc.vector.tensor_copy(
+                out=tgrp[:].rearrange("p (e i) j -> p e j i", i=4), in_=DXZ[(c, hf)][:].rearrange("p j (e i) -> p e j i", i=4)
+            )
             return tgrp
 
         def quantize_tokens(c, hf, tgrp):
@@ -397,7 +399,8 @@ def tile_pvfc_v_kernel(tc, x, z, r, bias, arg, v, grad_out, out_0, out_1):
                 for dh in range(2):
                     grp = prep.tile([P, NB, 4], BF16, name="grp", bufs=2, align_bytes=64)
                     nc.vector.tensor_copy(
-                        out=grp[:], in_=RAW[key][:, :, NB * dh : NB * (dh + 1)].rearrange("p j d -> p d j")
+                        out=grp[:].rearrange("p (e i) j -> p e j i", i=4),
+                        in_=RAW[key][:, :, NB * dh : NB * (dh + 1)].rearrange("p j (e i) -> p e j i", i=4),
                     )
                     halves.append(grp)
                 return halves

from contextlib import ExitStack

import concourse.mybir as mybir
from concourse.masks import make_identity

B, D, OUT = 1024, 1024, 2048
FLOPS = 2 * 2 * B * D * OUT

F32 = mybir.dt.float32
BF16 = mybir.dt.bfloat16
U32 = mybir.dt.uint32
U8 = mybir.dt.uint8
E4M3 = mybir.dt.float8_e4m3fn_x4
E5M2 = mybir.dt.float8_e5m2_x4
ALU = mybir.AluOpType
ACT = mybir.ActivationFunctionType
AX = mybir.AxisListType

P = 128
CH = 512
NCH = OUT // CH
NB = 512
BLK = 136
AHEAD = 3
TAIL_BANKS = 7


def tile_pvfc_v_kernel(tc, x, z, r, bias, arg, v, grad_out, out_0, out_1):
    nc = tc.nc
    arg_v = arg.rearrange("(g p j) o -> g p j o", g=2, j=4)
    v_v = v.rearrange("(g p j) o -> g p j o", g=2, j=4)
    go_v = grad_out.rearrange("(g p j) o -> g p j o", g=2, j=4)
    x_v = x.rearrange("(g p j) d -> g p j d", g=2, j=4)
    out0_v = out_0.rearrange("(g p j) d -> g p j d", g=2, j=4)
    z_k = z.rearrange("(c p j) d -> c p j d", c=NCH, j=4)
    z_rows = z.rearrange("(c m p) d -> c p m d", c=NCH, m=4)
    out1_v = out_1.rearrange("(c m p) d -> c p m d", c=NCH, m=4)

    with ExitStack() as ctx:
        ctx.enter_context(tc.manual_schedule())
        keep = ctx.enter_context(tc.tile_pool(name="keep", bufs=1))
        ring = ctx.enter_context(tc.tile_pool(name="ring", bufs=2))
        psum = ctx.enter_context(tc.psum_pool(name="psum", bufs=1))

        ident = keep.tile([P, P], F32, name="ident")
        make_identity(nc, ident[:])
        ones = keep.tile([P, 1], F32, name="ones")
        nc.vector.memset(ones[:], 1.0)
        warm = keep.tile([P, 1], F32, name="warm")
        nc.scalar.activation(out=warm[:], in_=ones[:], func=ACT.Sqrt)

        x_codes = keep.tile([P, 2, D], U32, name="x_codes", align_bytes=64)
        x_scales = keep.tile([P, 2, D], U8, name="x_scales", align_bytes=64)
        z_codes = keep.tile([P, NCH, D], U32, name="z_codes", align_bytes=64)
        z_scales = keep.tile([P, NCH, D], U8, name="z_scales", align_bytes=64)
        f_codes = keep.tile([P, NCH, B], U32, name="f_codes", align_bytes=64)
        f_scales = keep.tile([P, NCH, B], U8, name="f_scales", align_bytes=64)
        r_rows = keep.tile([P, OUT], BF16, name="r_rows")

        xsq_v = keep.tile([P, 4], F32, name="xsq_v")
        xsq_s = keep.tile([P, 4], F32, name="xsq_s")
        beta = keep.tile([P, 8], F32, name="beta")
        rbeta = keep.tile([P, 8], F32, name="rbeta")
        zsq = keep.tile([P, 4 * NCH], F32, name="zsq")
        zn = keep.tile([P, 4 * NCH], F32, name="zn")
        rzn = keep.tile([P, 4 * NCH], F32, name="rzn")
        sh2n = keep.tile([P, 4 * NCH], F32, name="sh2n")
        dbeta_part = keep.tile([P, 8, NCH], F32, name="dbeta_part")
        dbeta_over_beta = keep.tile([P, 8], F32, name="dbeta_over_beta")
        sums_s = keep.tile([P, 2 * NCH, 8], F32, name="sums_s")
        sums_v = keep.tile([P, 2 * NCH, 8], F32, name="sums_v")

        A, V, G, Q, M, W, EM, SG = {}, {}, {}, {}, {}, {}, {}, {}
        ER, C2, SH2, ZS2, ZROW, XROW = {}, {}, {}, {}, {}, {}
        DXZ, FGRP, TP, HA, YS, T_CODES, T_SCALES, ACC, STAGE, TZ, SHCOL = {}, {}, {}, {}, {}, {}, {}, {}, {}, {}, {}
        tail = []

        def cols(c):
            return slice(CH * c, CH * (c + 1))

        def blocks(t):
            return t[:].rearrange("p j (m o) -> p j m o", m=4)

        def load_arg(c, k):
            A[(c, k)] = ring.tile([P, 2, 4, BLK], F32, name="A", bufs=6)
            for jj in range(2):
                nc.sync.dma_start(
                    out=A[(c, k)][:, jj, :, 0:P],
                    in_=arg_v[k // 2][:, 2 * (k % 2) + jj, cols(c)].rearrange("p (m o) -> p m o", m=4),
                )

        def put_beta(c, k):
            nc.gpsimd.tensor_copy(
                out=A[(c, k)][:, :, :, P : P + 1],
                in_=beta[:, 2 * k : 2 * k + 2].unsqueeze(2).unsqueeze(3).to_broadcast([P, 2, 4, 1]),
            )

        def load_v_g(c, k):
            V[(c, k)] = ring.tile([P, 2, CH], F32, name="V", bufs=4)
            nc.sync.dma_start(out=V[(c, k)][:], in_=v_v[k // 2][:, 2 * (k % 2) : 2 * (k % 2) + 2, cols(c)])
            G[(c, k)] = ring.tile([P, 2, CH], BF16, name="G", bufs=4)
            nc.sync.dma_start(out=G[(c, k)][:], in_=go_v[k // 2][:, 2 * (k % 2) : 2 * (k % 2) + 2, cols(c)])

        def load_z_rows(c):
            for m in range(4):
                ZROW[(c, m)] = ring.tile([P, D], BF16, name="ROW", bufs=4)
                nc.sync.dma_start(out=ZROW[(c, m)][:], in_=z_rows[c][:, m, :])

        def sqrt_phase(c, k):
            Q[(c, k)] = ring.tile([P, 2, CH], F32, name="Q", bufs=6)
            W[(c, k)] = ring.tile([P, 2, CH], F32, name="W", bufs=2)
            M[(c, k)] = ring.tile([P, 2, CH], F32, name="M", bufs=6)
            nc.scalar.activation(out=blocks(Q[(c, k)]), in_=A[(c, k)][:, :, :, 0:P], func=ACT.Square)
            nc.scalar.activation(out=blocks(M[(c, k)]), in_=A[(c, k)][:, :, :, 0:P], func=ACT.Abs)
            nc.scalar.activation(out=W[(c, k)][:], in_=Q[(c, k)][:], func=ACT.Sqrt, bias=ones[:])

        def add_abs_w(c, k):
            nc.vector.tensor_tensor(out=M[(c, k)][:], in0=M[(c, k)][:], in1=W[(c, k)][:], op=ALU.add)

        def zn_phase(c):
            for m in range(4):
                nc.scalar.activation(
                    out=ZROW[(c, m)][:], in_=ZROW[(c, m)][:], func=ACT.Square, accum_out=zsq[:, 4 * c + m : 4 * c + m + 1]
                )
            nc.scalar.activation(out=zn[:, 4 * c : 4 * c + 4], in_=zsq[:, 4 * c : 4 * c + 4], func=ACT.Sqrt)

        def rsqrt_phase(c, k):
            nc.scalar.activation(out=Q[(c, k)][:], in_=Q[(c, k)][:], func=ACT.Abs_reciprocal_sqrt, bias=ones[:])

        def ln_phase(c, k):
            nc.scalar.activation(out=M[(c, k)][:], in_=M[(c, k)][:], func=ACT.Ln)

        def exp_r(c):
            ER[(c, 0)] = ring.tile([P, CH], F32, name="ER0", bufs=1)
            ER[(c, 1)] = ring.tile([P, CH], F32, name="ER1", bufs=1)
            nc.scalar.activation(out=ER[(c, 0)][:], in_=r_rows[:, cols(c)], func=ACT.Exp)
            nc.scalar.activation(out=ER[(c, 1)][:], in_=r_rows[:, cols(c)], func=ACT.Exp, scale=-1.0)

        def exp_phase(c, hf):
            for k in (2 * hf, 2 * hf + 1):
                EM[(c, k)] = ring.tile([P, 2, CH], F32, name="EM", bufs=2)
                nc.scalar.activation(out=EM[(c, k)][:], in_=V[(c, k)][:], func=ACT.Exp, scale=-1.0)
            for k in (2 * hf, 2 * hf + 1):
                nc.scalar.activation(out=V[(c, k)][:], in_=V[(c, k)][:], func=ACT.Exp)

        def sign_phase(c, k):
            SG[(c, k)] = ring.tile([P, 2, CH], BF16, name="SG", bufs=4)
            nc.scalar.activation(out=blocks(SG[(c, k)]), in_=A[(c, k)][:, :, :, 0:P], func=ACT.Sign)

        def zn_to_rows(c):
            zrow = psum.tile([P, NB], F32, name="acc", bufs=AHEAD)
            for m in range(4):
                nc.tensor.matmul(
                    out=zrow[:, P * m : P * (m + 1)], lhsT=zn[:, 4 * c + m : 4 * c + m + 1].to_broadcast([P, P]),
                    rhs=ident[:], start=True, stop=True,
                )
            return zrow

        def feature_rows(c, zrow):
            C2[c] = ring.tile([P, CH], F32, name="C2", bufs=1)
            SH2[c] = ring.tile([P, CH], F32, name="SH2", bufs=1)
            ZS2[c] = ring.tile([P, CH], F32, name="ZS2", bufs=1)
            nc.vector.tensor_tensor(out=C2[c][:], in0=ER[(c, 0)][:], in1=ER[(c, 1)][:], op=ALU.add)
            nc.vector.tensor_tensor(out=SH2[c][:], in0=ER[(c, 1)][:], in1=ER[(c, 0)][:], op=ALU.subtract)
            nc.vector.reciprocal(out=rzn[:, 4 * c : 4 * c + 4], in_=zn[:, 4 * c : 4 * c + 4])
            nc.vector.tensor_tensor(out=ZS2[c][:], in0=zrow[:], in1=SH2[c][:], op=ALU.mult)

        def sinh_to_partitions(c):
            SHCOL[c] = psum.tile([P, NB], F32, name="acc", bufs=AHEAD)
            for m in range(4):
                nc.tensor.matmul(
                    out=SHCOL[c][:, m : m + 1], lhsT=SH2[c][:, P * m : P * (m + 1)], rhs=ident[:, 0:1],
                    start=True, stop=True,
                )

        def copy_sinh(c):
            nc.scalar.copy(out=sh2n[:, 4 * c : 4 * c + 4], in_=SHCOL[c][:, 0:4])

        def chain_steps(c, k):
            hf, jp = k // 2, k % 2
            vv, q, mm = V[(c, k)], Q[(c, k)], M[(c, k)]

            def dbeta_step(jj):
                scrap = late.tile([P, CH], BF16, name="scrap", bufs=2)
                nc.vector.scalar_tensor_tensor(
                    out=scrap[:], in0=q[:, jj, :], scalar=1.0, in1=ZS2[c][:], op0=ALU.mult, op1=ALU.mult,
                    accum_out=dbeta_part[:, 4 * hf + 2 * jp + jj, c : c + 1],
                )

            return [
                lambda: nc.vector.tensor_tensor(out=vv[:], in0=vv[:], in1=EM[(c, k)][:], op=ALU.add),
                lambda: nc.vector.scalar_tensor_tensor(
                    out=vv[:], in0=vv[:], scalar=0.25, in1=G[(c, k)][:], op0=ALU.mult, op1=ALU.mult
                ),
                lambda: nc.vector.tensor_tensor(out=q[:], in0=vv[:], in1=q[:], op=ALU.mult),
                lambda: nc.vector.tensor_tensor(
                    out=DXZ[(c, hf)][:, 2 * jp : 2 * jp + 2, :], in0=q[:],
                    in1=C2[c][:].unsqueeze(1).to_broadcast([P, 2, CH]), op=ALU.mult,
                ),
                lambda: nc.vector.tensor_tensor(out=mm[:], in0=vv[:], in1=mm[:], op=ALU.mult),
                lambda: dbeta_step(0),
                lambda: nc.vector.tensor_tensor(out=mm[:], in0=mm[:], in1=SG[(c, k)][:], op=ALU.mult),
                lambda: dbeta_step(1),
            ]

        def chain(c, hf, first, last, between):
            if first == 0:
                DXZ[(c, hf)] = late.tile([P, 4, CH], BF16, name="DXZ", bufs=2)
            even, odd = chain_steps(c, 2 * hf), chain_steps(c, 2 * hf + 1)
            for i in range(first, last):
                even[i]()
                if between is not None:
                    between(2 * (i - 3))
                odd[i]()
                if between is not None:
                    between(2 * (i - 3) + 1)

        def h_arg_products(c, hf):
            for m in range(4):
                if m % 2 == 0:
                    bank = psum.tile([P, NB], F32, name="ha", bufs=2)
                    HA[(c, hf, m // 2)] = bank[:, 0 : 2 * BLK].rearrange("p (m w) -> p m w", m=2)
                for j in range(4):
                    k = 2 * hf + j // 2
                    nc.tensor.matmul(
                        out=HA[(c, hf, m // 2)][:, m % 2, 0 : P + 1], lhsT=Q[(c, k)][:, j % 2, P * m : P * (m + 1)],
                        rhs=A[(c, k)][:, j % 2, m, 0 : P + 1], start=(j == 0), stop=(j == 3),
                    )

        def y_sums(c, hf):
            YS[(c, hf)] = psum.tile([P, 16], F32, name="ys", bufs=1)
            for m in range(4):
                for j in range(4):
                    k = 2 * hf + j // 2
                    nc.tensor.matmul(
                        out=YS[(c, hf)][:, m : m + 1], lhsT=M[(c, k)][:, j % 2, P * m : P * (m + 1)], rhs=ones[:],
                        start=(j == 0), stop=(j == 3),
                    )

        def transposes(c, hf):
            for jp in range(2):
                TP[(c, hf, jp)] = psum.tile([P, 4, P], F32, name="tp", bufs=2)
                for jj in range(2):
                    words = DXZ[(c, hf)][:, 2 * jp + jj, :].bitcast(F32)
                    for u in range(2):
                        nc.tensor.transpose(out=TP[(c, hf, jp)][:, 2 * jj + u, :], in_=words[:, u::2], identity=ident[:])

        def copy_transposed(c, hf):
            FGRP[(c, hf)] = late.tile([P, CH, 4], BF16, name="FGRP", bufs=1, align_bytes=64)
            words = FGRP[(c, hf)][:].rearrange("p t e -> p (t e)").bitcast(F32).rearrange("p (j r u) -> p j r u", j=4, u=2)
            for jp in range(2):
                nc.scalar.copy(
                    out=words[:, 2 * jp : 2 * jp + 2, :, :], in_=TP[(c, hf, jp)][:].rearrange("p (jj u) r -> p jj r u", u=2)
                )

        def group_tokens(c, hf):
            if hf == 0:
                T_CODES[c] = ring.tile([P, 2, CH], U32, name="T_CODES", bufs=2, align_bytes=64)
                T_SCALES[c] = ring.tile([P, 2, CH], U8, name="T_SCALES", bufs=2, align_bytes=64)
            tgrp = late.tile([P, CH, 4], BF16, name="TGRP", bufs=1, align_bytes=64)
            nc.vector.tensor_copy(
                out=tgrp[:].rearrange("p (e i) j -> p e j i", i=4), in_=DXZ[(c, hf)][:].rearrange("p j (e i) -> p e j i", i=4)
            )
            return tgrp

        def quantize_tokens(c, hf, tgrp):
            nc.vector.quantize_mx(
                out=T_CODES[c][:, hf, :].bitcast(E5M2), scales=T_SCALES[c][:, hf, :],
                in_=tgrp[:].rearrange("p o j -> p (o j)"),
            )

        def quantize_features(c, hf):
            nc.vector.quantize_mx(
                out=f_codes[:, c, CH * hf : CH * (hf + 1)].bitcast(E5M2), scales=f_scales[:, c, CH * hf : CH * (hf + 1)],
                in_=FGRP[(c, hf)][:].rearrange("p t e -> p (t e)"),
            )

        def read_h_arg(c, hf):
            for m in range(4):
                scrap = late.tile([P, P], F32, name="scrap_d", bufs=4)
                nc.vector.scalar_tensor_tensor(
                    out=scrap[:], in0=HA[(c, hf, m // 2)][:, m % 2, 0:P], scalar=1.0, in1=ident[:], op0=ALU.mult,
                    op1=ALU.mult, accum_out=sums_v[:, 2 * c + hf, m : m + 1],
                )
            for mp in range(2):
                nc.scalar.copy(
                    out=sums_s[:, 2 * c + hf, 4 + 2 * mp : 6 + 2 * mp],
                    in_=HA[(c, hf, mp)][:, :, P : P + 1].rearrange("p m one -> p (m one)"),
                )

        def read_y_sums(c, hf):
            nc.scalar.copy(out=sums_s[:, 2 * c + hf, 0:4], in_=YS[(c, hf)][:, 0:4])

        def t_over_zn(c):
            both = keep.tile([P, 8], F32, name="both", bufs=2)
            harg = keep.tile([P, 4], F32, name="harg", bufs=2)
            ta = keep.tile([P, 4], F32, name="ta", bufs=2)
            tb = keep.tile([P, 4], F32, name="tb", bufs=2)
            TZ[c] = keep.tile([P, 4], F32, name="tz", bufs=2)
            nc.gpsimd.tensor_tensor(out=both[:], in0=sums_s[:, 2 * c, :], in1=sums_s[:, 2 * c + 1, :], op=ALU.add)
            nc.gpsimd.tensor_tensor(out=harg[:], in0=sums_v[:, 2 * c, 0:4], in1=sums_v[:, 2 * c + 1, 0:4], op=ALU.add)
            nc.gpsimd.tensor_tensor(out=ta[:], in0=both[:, 0:4], in1=harg[:], op=ALU.subtract)
            nc.gpsimd.tensor_tensor(out=tb[:], in0=both[:, 4:8], in1=sh2n[:, 4 * c : 4 * c + 4], op=ALU.mult)
            nc.gpsimd.tensor_tensor(out=ta[:], in0=ta[:], in1=ta[:], op=ALU.add)
            nc.gpsimd.tensor_tensor(out=ta[:], in0=ta[:], in1=tb[:], op=ALU.add)
            nc.gpsimd.tensor_tensor(out=TZ[c][:], in0=ta[:], in1=rzn[:, 4 * c : 4 * c + 4], op=ALU.mult)

        def accumulator():
            if len(tail) == 0:
                return psum.tile([P, NB], F32, name="acc", bufs=AHEAD)
            turn = (len(tail) - 1) % TAIL_BANKS
            tail.append(0)
            if turn < AHEAD:
                return psum.tile([P, NB], F32, name="acc", bufs=AHEAD)
            if turn < AHEAD + 2:
                bank = psum.tile([P, 4, P], F32, name="tp", bufs=2)
                return bank[:].rearrange("p a b -> p (a b)")
            return psum.tile([P, NB], F32, name="ha", bufs=2)

        def staging():
            if len(tail) == 0:
                return late.tile([P, D], F32, name="stage", bufs=2)
            row = ring.tile([P, 2, CH], F32, name="Q", bufs=6)
            return row[:].rearrange("p a b -> p (a b)")

        def out1_product(c, i):
            m, dh = i // 2, i % 2
            ACC[("out1", c, i)] = accumulator()
            for g in range(2):
                nc.tensor.matmul_mx(
                    out=ACC[("out1", c, i)][:],
                    lhsT=T_CODES[c][:, g, P * m : P * (m + 1)].bitcast(E5M2),
                    lhsT_scale=T_SCALES[c][:, g, P * m : P * (m + 1)],
                    rhs=x_codes[:, g, NB * dh : NB * (dh + 1)].bitcast(E4M3),
                    rhs_scale=x_scales[:, g, NB * dh : NB * (dh + 1)],
                    start=(g == 0), stop=(g == 1),
                )

        def out1_epilogue(c, i):
            m, dh = i // 2, i % 2
            if dh == 0:
                STAGE[("out1", c, m)] = staging()
            row = STAGE[("out1", c, m)]
            nc.vector.scalar_tensor_tensor(
                out=row[:, NB * dh : NB * (dh + 1)], in0=ZROW[(c, m)][:, NB * dh : NB * (dh + 1)],
                scalar=TZ[c][:, m : m + 1], in1=ACC[("out1", c, i)][:], op0=ALU.mult, op1=ALU.add,
            )
            if dh == 1:
                nc.sync.dma_start(out=out1_v[c][:, m, :], in_=row[:])

        def load_x_row(g, j):
            XROW[(g, j)] = late.tile([P, D], BF16, name="XROW", bufs=2)
            nc.sync.dma_start(out=XROW[(g, j)][:], in_=x_v[g][:, j, :])

        def out0_factor(g):
            total = keep.tile([P, 4], F32, name="total", bufs=2)
            nc.vector.tensor_reduce(out=total[:], in_=dbeta_part[:, 4 * g : 4 * g + 4, :], axis=AX.X, op=ALU.add)
            nc.vector.tensor_tensor(
                out=dbeta_over_beta[:, 4 * g : 4 * g + 4], in0=total[:], in1=rbeta[:, 4 * g : 4 * g + 4], op=ALU.mult
            )

        def out0_product(g, i):
            s, dh = 4 * g + i // 2, i % 2
            ACC[("out0", g, i)] = accumulator()
            for c in range(NCH):
                nc.tensor.matmul_mx(
                    out=ACC[("out0", g, i)][:],
                    lhsT=f_codes[:, c, P * s : P * (s + 1)].bitcast(E5M2),
                    lhsT_scale=f_scales[:, c, P * s : P * (s + 1)],
                    rhs=z_codes[:, c, NB * dh : NB * (dh + 1)].bitcast(E4M3),
                    rhs_scale=z_scales[:, c, NB * dh : NB * (dh + 1)],
                    start=(c == 0), stop=(c == NCH - 1),
                )

        def out0_epilogue(g, i):
            j, dh = i // 2, i % 2
            if dh == 0:
                STAGE[("out0", g, j)] = staging()
            row = STAGE[("out0", g, j)]
            nc.vector.scalar_tensor_tensor(
                out=row[:, NB * dh : NB * (dh + 1)], in0=XROW[(g, j)][:, NB * dh : NB * (dh + 1)],
                scalar=dbeta_over_beta[:, 4 * g + j : 4 * g + j + 1], in1=ACC[("out0", g, i)][:],
                op0=ALU.mult, op1=ALU.add,
            )
            if dh == 1:
                nc.sync.dma_start(out=out0_v[g][:, j, :], in_=row[:])
                if j + 2 < 4:
                    load_x_row(g, j + 2)

        with tc.tile_pool(name="prep", bufs=2) as prep:
            RAW = {}

            def load_raw(key, src):
                RAW[key] = prep.tile([P, 4, D], BF16, name="raw", bufs=2)
                nc.sync.dma_start(out=RAW[key][:], in_=src)

            def group_rows(key):
                halves = []
                for dh in range(2):
                    grp = prep.tile([P, NB, 4], BF16, name="grp", bufs=2, align_bytes=64)
                    nc.vector.tensor_copy(
                        out=grp[:].rearrange("p (e i) j -> p e j i", i=4),
                        in_=RAW[key][:, :, NB * dh : NB * (dh + 1)].rearrange("p j (e i) -> p e j i", i=4),
                    )
                    halves.append(grp)
                return halves

            def quantize_rows(halves, codes, scales):
                for dh in range(2):
                    nc.vector.quantize_mx(
                        out=codes[:, NB * dh : NB * (dh + 1)].bitcast(E4M3), scales=scales[:, NB * dh : NB * (dh + 1)],
                        in_=halves[dh][:].rearrange("p d j -> p (d j)"),
                    )

            load_arg(0, 0)
            load_arg(0, 1)
            load_raw(("x", 0), x_v[0])
            load_arg(0, 2)
            load_arg(0, 3)
            load_raw(("x", 1), x_v[1])
            load_z_rows(0)
            nc.sync.dma_start(out=r_rows[:], in_=r.rearrange("o one -> (o one)").partition_broadcast(P))
            for k in range(4):
                load_v_g(0, k)
            sqrt_phase(0, 0)
            sqrt_phase(0, 1)
            x0 = group_rows(("x", 0))
            add_abs_w(0, 0)
            add_abs_w(0, 1)
            sqrt_phase(0, 2)
            sqrt_phase(0, 3)
            for j in range(4):
                scrap = prep.tile([P, D], BF16, name="scrap_x", bufs=2)
                nc.vector.scalar_tensor_tensor(
                    out=scrap[:], in0=RAW[("x", 0)][:, j, :], scalar=1.0, in1=RAW[("x", 0)][:, j, :],
                    op0=ALU.mult, op1=ALU.mult, accum_out=xsq_v[:, j : j + 1],
                )
            zn_phase(0)
            nc.scalar.activation(out=beta[:, 0:4], in_=xsq_v[:], func=ACT.Sqrt, bias=ones[:])
            put_beta(0, 0)
            put_beta(0, 1)
            quantize_rows(x0, x_codes[:, 0, :], x_scales[:, 0, :])
            load_raw(("z", 0), z_k[0])
            add_abs_w(0, 2)
            add_abs_w(0, 3)
            for k in range(4):
                rsqrt_phase(0, k)
            for k in range(4):
                ln_phase(0, k)
            exp_r(0)
            exp_phase(0, 0)
            sign_phase(0, 0)
            sign_phase(0, 1)
            for j in range(4):
                xrow = ring.tile([P, D], BF16, name="ROW", bufs=4)
                nc.sync.dma_start(out=xrow[:], in_=x_v[1][:, j, :])
                nc.scalar.activation(out=xrow[:], in_=xrow[:], func=ACT.Square, accum_out=xsq_s[:, j : j + 1])
            x1 = group_rows(("x", 1))
            quantize_rows(x1, x_codes[:, 1, :], x_scales[:, 1, :])
            load_raw(("z", 1), z_k[1])
            for c in range(NCH):
                zc = group_rows(("z", c))
                if c + 2 < NCH:
                    load_raw(("z", c + 2), z_k[c + 2])
                quantize_rows(zc, z_codes[:, c, :], z_scales[:, c, :])
            load_arg(1, 0)
            load_arg(1, 1)

        late = ctx.enter_context(tc.tile_pool(name="late", bufs=2))
        feature_rows(0, zn_to_rows(0))
        sinh_to_partitions(0)
        copy_sinh(0)

        last = 2 * NCH - 1
        for n in range(2 * NCH):
            c, hf = n // 2, n % 2
            nx = c + 1
            more = nx < NCH
            pc, ph = (n - 1) // 2, (n - 1) % 2

            if hf == 0 and c >= 1:
                product, epilogue = (lambda i: out1_product(c - 1, i)), (lambda i: out1_epilogue(c - 1, i))
                groups = 8
            elif n == last:
                product, epilogue = (lambda i: out0_product(0, i)), (lambda i: out0_epilogue(0, i))
                groups = 8
            else:
                product, epilogue = None, None
                groups = 0

            def woven(place):
                i = place if place < AHEAD else place - 2
                if i < groups and place != AHEAD and place != AHEAD + 1:
                    epilogue(i)
                    if i + AHEAD < groups:
                        product(i + AHEAD)

            if n >= 1:
                read_h_arg(pc, ph)
                if hf == 0:
                    copy_sinh(c)
            for i in range(min(AHEAD, groups)):
                product(i)
            chain(c, hf, 0, 1, None)
            if n >= 1:
                read_y_sums(pc, ph)
                if hf == 0:
                    t_over_zn(pc)
            chain(c, hf, 1, 3, None)
            if hf == 0:
                exp_phase(c, 1)
                sign_phase(c, 2)
                sign_phase(c, 3)
                if more:
                    exp_r(nx)
            if n == 0:
                nc.scalar.activation(out=beta[:, 4:8], in_=xsq_s[:], func=ACT.Sqrt, bias=ones[:])
                put_beta(0, 2)
                put_beta(0, 3)
                put_beta(1, 0)
                put_beta(1, 1)
            h_arg_products(c, hf)
            if more and hf == 0:
                sqrt_phase(nx, 0)
                sqrt_phase(nx, 1)
                load_arg(nx, 2)
                load_arg(nx, 3)
                put_beta(nx, 2)
                put_beta(nx, 3)
            if more and hf == 1:
                add_abs_w(nx, 2)
                add_abs_w(nx, 3)
                zrow = zn_to_rows(nx)
                for k in range(4):
                    rsqrt_phase(nx, k)
                if nx + 1 < NCH:
                    load_arg(nx + 1, 0)
                    load_arg(nx + 1, 1)
                    put_beta(nx + 1, 0)
                    put_beta(nx + 1, 1)
            if n == last:
                chain(c, hf, 3, 4, woven)
                transposes(c, hf)
                copy_transposed(c, hf)
                chain(c, hf, 4, 8, woven)
                y_sums(c, hf)
            else:
                chain(c, hf, 3, 8, woven)
                y_sums(c, hf)
                if n >= 1:
                    copy_transposed(pc, ph)
                transposes(c, hf)
            if n == 0:
                nc.vector.reciprocal(out=rbeta[:], in_=beta[:])
            if more and hf == 0:
                load_v_g(nx, 0)
                load_v_g(nx, 1)
                load_z_rows(nx)
                add_abs_w(nx, 0)
                add_abs_w(nx, 1)
                sqrt_phase(nx, 2)
                sqrt_phase(nx, 3)
                zn_phase(nx)
            if more and hf == 1:
                for k in range(4):
                    ln_phase(nx, k)
                load_v_g(nx, 2)
                load_v_g(nx, 3)
                exp_phase(nx, 0)
                sign_phase(nx, 0)
                sign_phase(nx, 1)
            tgrp = group_tokens(c, hf)
            if n >= 1 and n != last:
                quantize_features(pc, ph)
            quantize_tokens(c, hf, tgrp)
            if hf == 1:
                if more:
                    feature_rows(nx, zrow)
                    sinh_to_partitions(nx)
                load_z_rows(c)
            if n == last - 1:
                load_x_row(0, 0)
                load_x_row(0, 1)
                copy_transposed(c, hf)
                quantize_features(c, hf)
                out0_factor(0)

        load_x_row(1, 0)
        load_x_row(1, 1)
        quantize_features(NCH - 1, 1)
        out0_factor(1)
        read_h_arg(NCH - 1, 1)
        read_y_sums(NCH - 1, 1)
        t_over_zn(NCH - 1)
        tail.append(0)

        def tail_product(i):
            if i < 8:
                out0_product(1, i)
            else:
                out1_product(NCH - 1, i - 8)

        for i in range(TAIL_BANKS):
            tail_product(i)
        for i in range(16):
            if i < 8:
                out0_epilogue(1, i)
            else:
                out1_epilogue(NCH - 1, i - 8)
            if i + TAIL_BANKS < 16:
                tail_product(i + TAIL_BANKS)
